import numpy as np
import ml_dtypes


def mxq(x, axis, fmt="e4m3"):
    dtype, down = {"e4m3": (ml_dtypes.float8_e4m3fn, 7), "e5m2": (ml_dtypes.float8_e5m2, 14)}[fmt]
    v = np.moveaxis(np.asarray(x, np.float32).astype(ml_dtypes.bfloat16).astype(np.float64), axis, -1)
    blocks = v.reshape(v.shape[:-1] + (-1, 32))
    amax = np.abs(blocks).max(-1, keepdims=True)
    byte = np.maximum(np.where(amax > 0, np.frexp(amax)[1] - 1 + 127, 0) - down, 1)
    scale = np.exp2(byte - 127.0)
    codes = (blocks / scale).astype(np.float32).astype(dtype).astype(np.float64)
    return np.moveaxis((codes * scale).reshape(v.shape), -1, axis)


WIDE = False


def mx_kscale(k):
    if not WIDE:
        return np.ones(k)
    levels = np.array([10, -10, 5, -5, 0])
    a = np.random.permutation(np.resize(levels, k // 512 * 4)).reshape(k // 512, 4)
    idx = np.arange(k)
    return np.exp2(a[idx // 512, idx % 128 // 32])


BF16 = ml_dtypes.bfloat16


def bf(x):
    return np.asarray(x, np.float32).astype(BF16)


def f64(x):
    return np.asarray(x).astype(np.float64)


B, C, CI, N = 2, 1024, 512, 1024
A = np.sqrt(0.2 * N / np.sqrt(CI))


def conv1x1(w, b, v):
    return (mxq(w, 1, "e4m3") @ mxq(v, 1, "e4m3")) + b[:, None]


def setup_inputs():
    s, u, t = mx_kscale(C), mx_kscale(C), mx_kscale(CI)
    r = np.random.standard_normal
    return {"x": bf(r((B, C, N)) * s[None, :, None]),
            "x_2": bf(r((B, C, N)) * u[None, :, None]),
            "theta_w": bf(r((CI, C)) * A / np.sqrt(C) * t[:, None] / s[None, :]),
            "theta_b": bf(r(CI) * 0.2 * A * t),
            "phi_w": bf(r((CI, C)) * A / np.sqrt(C) / t[:, None] / u[None, :]),
            "phi_b": bf(r(CI) * 0.2 * A / t)}


def reference(x, x_2, theta_w, theta_b, phi_w, phi_b):
    theta_x = conv1x1(f64(theta_w), f64(theta_b), f64(x)).transpose(0, 2, 1)
    phi_x = conv1x1(f64(phi_w), f64(phi_b), f64(x_2))
    return (mxq(theta_x, 2, "e4m3") @ mxq(phi_x, 1, "e4m3")) / N

@@ -1,0 +1,169 @@
+from contextlib import ExitStack
+
+import concourse.mybir as mybir
+from concourse.masks import make_identity
+
+FP8X4 = mybir.dt.float8_e4m3fn_x4
+BF16 = mybir.dt.bfloat16
+F32 = mybir.dt.float32
+U32 = mybir.dt.uint32
+U8 = mybir.dt.uint8
+IDENTITY = mybir.ActivationFunctionType.Identity
+
+BATCH, CHANNELS, INNER, POINTS = 2, 1024, 512, 1024
+
+P = 128
+PACK = 4
+K_PASS = P * PACK
+PASSES = CHANNELS // K_PASS
+PIECE = 512
+PIECES = POINTS // PIECE
+WORD = 2
+
+FLOPS = 2 * BATCH * (2 * INNER * CHANNELS * POINTS + POINTS * POINTS * INNER)
+
+
+def side_by_side(rows_apart, together):
+    return (
+        together.rearrange("p (g i) j -> p g j i", i=4),
+        rows_apart.rearrange("p j (g i) -> p g j i", i=4),
+    )
+
+
+def load_points(nc, pool, points, name):
+    raw = pool.tile([P, PASSES, PACK, POINTS], BF16, name=name)
+    for c in range(PASSES):
+        rows = points[c * K_PASS : (c + 1) * K_PASS, :]
+        nc.sync.dma_start(out=raw[:, c], in_=rows.rearrange("(p j) n -> p j n", j=PACK))
+    return raw
+
+
+def load_weights(nc, pool, w, b, name):
+    w_raw = pool.tile([P, PACK, CHANNELS], BF16, name="%s_raw" % name)
+    nc.sync.dma_start(out=w_raw[:], in_=w.rearrange("(m t) k -> m t k", t=PACK))
+    bias_bf16 = pool.tile([P, PACK], BF16, name="%s_bias_bf16" % name)
+    nc.scalar.dma_start(out=bias_bf16[:], in_=b.rearrange("(m t) -> m t", t=PACK))
+    bias = pool.tile([P, PACK], F32, name="%s_bias" % name)
+    nc.vector.tensor_copy(out=bias[:], in_=bias_bf16[:])
+    return w_raw, bias
+
+
+def quantise_weights(nc, pool, psum, identity, w_raw, name):
+    words = w_raw[:].bitcast(F32).rearrange("m t (c p u) -> m t c u p", c=PASSES, u=PACK // WORD)
+    grouped = pool.tile([P, PASSES, PACK, P, PACK], BF16, name="%s_grouped" % name, align_bytes=64)
+    grouped_words = grouped[:].bitcast(F32)
+    for t in range(PACK):
+        flipped = psum.tile([P, PASSES, PACK // WORD, P], F32, tag="bank")
+        for c in range(PASSES):
+            for u in range(PACK // WORD):
+                nc.tensor.transpose(flipped[:, c, u, :], words[:, t, c, u, :], identity[:])
+        nc.scalar.copy(out=grouped_words[:, :, t], in_=flipped[:].rearrange("p c u m -> p c m u"))
+    codes = pool.tile([P, PASSES, INNER], U32, name="%s_codes" % name, align_bytes=64)
+    scales = pool.tile([P, PASSES, INNER], U8, name="%s_scales" % name, align_bytes=64)
+    nc.vector.quantize_mx(
+        out=codes[:].rearrange("p c n -> p (c n)").bitcast(FP8X4),
+        scales=scales[:].rearrange("p c n -> p (c n)"),
+        in_=grouped[:].rearrange("p c t m j -> p (c t m j)"),
+    )
+    return codes, scales
+
+
+def quantise_points(nc, pool, raw, piece):
+    grouped = pool.tile([P, PASSES, PIECE, PACK], BF16, align_bytes=64)
+    for c in range(PASSES):
+        dst, src = side_by_side(raw[:, c, :, piece * PIECE : (piece + 1) * PIECE], grouped[:, c])
+        nc.vector.tensor_copy(out=dst, in_=src)
+    codes = pool.tile([P, PASSES, PIECE], U32, align_bytes=64)
+    scales = pool.tile([P, PASSES, PIECE], U8, align_bytes=64)
+    nc.vector.quantize_mx(
+        out=codes[:].rearrange("p c n -> p (c n)").bitcast(FP8X4),
+        scales=scales[:].rearrange("p c n -> p (c n)"),
+        in_=grouped[:].rearrange("p c n j -> p (c n j)"),
+    )
+    return codes, scales
+
+
+def project(nc, pool, keep, psum, weight, bias, points):
+    w_codes, w_scales = weight
+    x_codes, x_scales = points
+    projected = pool.tile([P, PACK, PIECE], BF16)
+    for t in range(PACK):
+        columns = slice(t * P, (t + 1) * P)
+        acc = psum.tile([P, PIECE], F32, tag="bank")
+        for c in range(PASSES):
+            nc.tensor.matmul_mx(
+                out=acc[:],
+                lhsT=w_codes[:, c, columns].bitcast(FP8X4),
+                lhsT_scale=w_scales[:, c, columns],
+                rhs=x_codes[:, c, :].bitcast(FP8X4),
+                rhs_scale=x_scales[:, c, :],
+                start=(c == 0),
+                stop=(c == PASSES - 1),
+            )
+        nc.scalar.activation(
+            out=projected[:, t, :], in_=acc[:], func=IDENTITY, bias=bias[:, t : t + 1], scale=1.0
+        )
+    grouped = pool.tile([P, PIECE, PACK], BF16, align_bytes=64)
+    dst, src = side_by_side(projected[:], grouped[:])
+    nc.vector.tensor_copy(out=dst, in_=src)
+    codes = keep.tile([P, PIECE], U32, align_bytes=64)
+    scales = keep.tile([P, PIECE], U8, align_bytes=64)
+    nc.vector.quantize_mx(
+        out=codes[:].bitcast(FP8X4), scales=scales[:], in_=grouped[:].rearrange("p n j -> p (n j)")
+    )
+    return codes, scales
+
+
+def affinity(nc, pool, psum, theta, phi, out_rows):
+    theta_codes, theta_scales = theta
+    for r in range(PIECE // P):
+        columns = slice(r * P, (r + 1) * P)
+        result = pool.tile([P, POINTS], F32)
+        for piece, (phi_codes, phi_scales) in enumerate(phi):
+            acc = psum.tile([P, PIECE], F32, tag="bank")
+            nc.tensor.matmul_mx(
+                out=acc[:],
+                lhsT=theta_codes[:, columns].bitcast(FP8X4),
+                lhsT_scale=theta_scales[:, columns],
+                rhs=phi_codes[:].bitcast(FP8X4),
+                rhs_scale=phi_scales[:],
+                start=True,
+                stop=True,
+            )
+            nc.scalar.mul(
+                out=result[:, piece * PIECE : (piece + 1) * PIECE], in_=acc[:], mul=1.0 / POINTS
+            )
+        nc.sync.dma_start(out=out_rows[columns, :], in_=result[:])
+
+
+def tile_sgcam_pa_kernel(tc, x, x_2, theta_w, theta_b, phi_w, phi_b, out):
+    nc = tc.nc
+    with ExitStack() as ctx:
+        resident = ctx.enter_context(tc.tile_pool(name="resident", bufs=1))
+        stage = ctx.enter_context(tc.tile_pool(name="stage", bufs=3))
+        keep = ctx.enter_context(tc.tile_pool(name="keep", bufs=6))
+        results = ctx.enter_context(tc.tile_pool(name="results", bufs=6))
+        psum = ctx.enter_context(tc.psum_pool(name="psum", bufs=8))
+
+        identity = resident.tile([P, P], F32)
+        make_identity(nc, identity[:])
+
+        phi_raw, phi_bias = load_weights(nc, resident, phi_w, phi_b, "phi")
+        x_2_raw = [load_points(nc, resident, x_2[0], "x_2_raw0")]
+        theta_raw, theta_bias = load_weights(nc, resident, theta_w, theta_b, "theta")
+        x_raw = [load_points(nc, resident, x[0], "x_raw0")]
+        x_2_raw.append(load_points(nc, resident, x_2[1], "x_2_raw1"))
+        x_raw.append(load_points(nc, resident, x[1], "x_raw1"))
+
+        phi_weight = quantise_weights(nc, resident, psum, identity, phi_raw, "phi")
+        theta_weight = quantise_weights(nc, resident, psum, identity, theta_raw, "theta")
+
+        for b in range(BATCH):
+            phi = []
+            for piece in range(PIECES):
+                points = quantise_points(nc, stage, x_2_raw[b], piece)
+                phi.append(project(nc, stage, keep, psum, phi_weight, phi_bias, points))
+            for piece in range(PIECES):
+                points = quantise_points(nc, stage, x_raw[b], piece)
+                theta = project(nc, stage, keep, psum, theta_weight, theta_bias, points)
+                affinity(nc, results, psum, theta, phi, out[b, piece * PIECE : (piece + 1) * PIECE, :])

@@ -16,9 +16,14 @@ P = 128
 PACK = 4
 K_PASS = P * PACK
 PASSES = CHANNELS // K_PASS
-PIECE = 512
-PIECES = POINTS // PIECE
 WORD = 2
+BANK = 512
+PIECE = 256
+PIECES = POINTS // PIECE
+LOAD = 512
+LAG = 2
+WEIGHT_LEAD = 2
+VECTOR_SHARE = 4
 
 FLOPS = 2 * BATCH * (2 * INNER * CHANNELS * POINTS + POINTS * POINTS * INNER)
 
@@ -32,9 +37,13 @@ def side_by_side(rows_apart, together):
 
 def load_points(nc, pool, points, name):
     raw = pool.tile([P, PASSES, PACK, POINTS], BF16, name=name)
-    for c in range(PASSES):
-        rows = points[c * K_PASS : (c + 1) * K_PASS, :]
-        nc.sync.dma_start(out=raw[:, c], in_=rows.rearrange("(p j) n -> p j n", j=PACK))
+    for first in range(0, POINTS, LOAD):
+        for c in range(PASSES):
+            rows = points[c * K_PASS : (c + 1) * K_PASS, first : first + LOAD]
+            nc.sync.dma_start(
+                out=raw[:, c, :, first : first + LOAD],
+                in_=rows.rearrange("(p j) n -> p j n", j=PACK),
+            )
     return raw
 
 
@@ -48,7 +57,7 @@ def load_weights(nc, pool, w, b, name):
     return w_raw, bias
 
 
-def quantise_weights(nc, pool, psum, identity, w_raw, name):
+def transpose_weights(nc, pool, psum, identity, w_raw, name):
     words = w_raw[:].bitcast(F32).rearrange("m t (c p u) -> m t c u p", c=PASSES, u=PACK // WORD)
     grouped = pool.tile([P, PASSES, PACK, P, PACK], BF16, name="%s_grouped" % name, align_bytes=64)
     grouped_words = grouped[:].bitcast(F32)
@@ -58,8 +67,12 @@ def quantise_weights(nc, pool, psum, identity, w_raw, name):
             for u in range(PACK // WORD):
                 nc.tensor.transpose(flipped[:, c, u, :], words[:, t, c, u, :], identity[:])
         nc.scalar.copy(out=grouped_words[:, :, t], in_=flipped[:].rearrange("p c u m -> p c m u"))
-    codes = pool.tile([P, PASSES, INNER], U32, name="%s_codes" % name, align_bytes=64)
-    scales = pool.tile([P, PASSES, INNER], U8, name="%s_scales" % name, align_bytes=64)
+    return grouped
+
+
+def quantise_weights(nc, pool, grouped, name):
+    codes = pool.tile([P, PASSES, INNER], U32, name="%s_w_codes" % name, align_bytes=64)
+    scales = pool.tile([P, PASSES, INNER], U8, name="%s_w_scales" % name, align_bytes=64)
     nc.vector.quantize_mx(
         out=codes[:].rearrange("p c n -> p (c n)").bitcast(FP8X4),
         scales=scales[:].rearrange("p c n -> p (c n)"),
@@ -68,24 +81,25 @@ def quantise_weights(nc, pool, psum, identity, w_raw, name):
     return codes, scales
 
 
-def quantise_points(nc, pool, raw, piece):
-    grouped = pool.tile([P, PASSES, PIECE, PACK], BF16, align_bytes=64)
-    for c in range(PASSES):
-        dst, src = side_by_side(raw[:, c, :, piece * PIECE : (piece + 1) * PIECE], grouped[:, c])
-        nc.vector.tensor_copy(out=dst, in_=src)
-    codes = pool.tile([P, PASSES, PIECE], U32, align_bytes=64)
-    scales = pool.tile([P, PASSES, PIECE], U8, align_bytes=64)
+def regroup_points(nc, raw, q, c, points_grouped):
+    dst, src = side_by_side(raw[:, c, :, q * PIECE : (q + 1) * PIECE], points_grouped[:, c])
+    nc.vector.tensor_copy(out=dst, in_=src)
+
+
+def quantise_points(nc, pool, points_grouped):
+    points_codes = pool.tile([P, PASSES, PIECE], U32, align_bytes=64)
+    points_scales = pool.tile([P, PASSES, PIECE], U8, align_bytes=64)
     nc.vector.quantize_mx(
-        out=codes[:].rearrange("p c n -> p (c n)").bitcast(FP8X4),
-        scales=scales[:].rearrange("p c n -> p (c n)"),
-        in_=grouped[:].rearrange("p c n j -> p (c n j)"),
+        out=points_codes[:].rearrange("p c n -> p (c n)").bitcast(FP8X4),
+        scales=points_scales[:].rearrange("p c n -> p (c n)"),
+        in_=points_grouped[:].rearrange("p c n j -> p (c n j)"),
     )
-    return codes, scales
+    return points_codes, points_scales
 
 
-def project(nc, pool, keep, psum, weight, bias, points):
+def project(nc, pool, psum, weight, bias, points):
     w_codes, w_scales = weight
-    x_codes, x_scales = points
+    points_codes, points_scales = points
     projected = pool.tile([P, PACK, PIECE], BF16)
     for t in range(PACK):
         columns = slice(t * P, (t + 1) * P)
@@ -95,75 +109,118 @@ def project(nc, pool, keep, psum, weight, bias, points):
                 out=acc[:],
                 lhsT=w_codes[:, c, columns].bitcast(FP8X4),
                 lhsT_scale=w_scales[:, c, columns],
-                rhs=x_codes[:, c, :].bitcast(FP8X4),
-                rhs_scale=x_scales[:, c, :],
+                rhs=points_codes[:, c, :].bitcast(FP8X4),
+                rhs_scale=points_scales[:, c, :],
                 start=(c == 0),
                 stop=(c == PASSES - 1),
             )
         nc.scalar.activation(
             out=projected[:, t, :], in_=acc[:], func=IDENTITY, bias=bias[:, t : t + 1], scale=1.0
         )
-    grouped = pool.tile([P, PIECE, PACK], BF16, align_bytes=64)
-    dst, src = side_by_side(projected[:], grouped[:])
+    return projected
+
+
+def regroup_projection(nc, pool, projected):
+    projected_grouped = pool.tile([P, PIECE, PACK], BF16, align_bytes=64)
+    dst, src = side_by_side(projected[:], projected_grouped[:])
     nc.vector.tensor_copy(out=dst, in_=src)
-    codes = keep.tile([P, PIECE], U32, align_bytes=64)
-    scales = keep.tile([P, PIECE], U8, align_bytes=64)
+    return projected_grouped
+
+
+def quantise_projection(nc, projected_grouped, quantised, q):
+    codes, scales = quantised
+    columns = slice(q * PIECE, (q + 1) * PIECE)
     nc.vector.quantize_mx(
-        out=codes[:].bitcast(FP8X4), scales=scales[:], in_=grouped[:].rearrange("p n j -> p (n j)")
+        out=codes[:, columns].bitcast(FP8X4),
+        scales=scales[:, columns],
+        in_=projected_grouped[:].rearrange("p n j -> p (n j)"),
     )
-    return codes, scales
 
 
-def affinity(nc, pool, psum, theta, phi, out_rows):
+def affinity(nc, pool, psum, theta, phi, q, out_b):
     theta_codes, theta_scales = theta
-    for r in range(PIECE // P):
-        columns = slice(r * P, (r + 1) * P)
+    phi_codes, phi_scales = phi
+    banks = 0
+    for first in range(q * PIECE, (q + 1) * PIECE, P):
         result = pool.tile([P, POINTS], F32)
-        for piece, (phi_codes, phi_scales) in enumerate(phi):
-            acc = psum.tile([P, PIECE], F32, tag="bank")
+        for columns in [slice(n, n + BANK) for n in range(0, POINTS, BANK)]:
+            acc = psum.tile([P, BANK], F32, tag="bank")
             nc.tensor.matmul_mx(
                 out=acc[:],
-                lhsT=theta_codes[:, columns].bitcast(FP8X4),
-                lhsT_scale=theta_scales[:, columns],
-                rhs=phi_codes[:].bitcast(FP8X4),
-                rhs_scale=phi_scales[:],
+                lhsT=theta_codes[:, first : first + P].bitcast(FP8X4),
+                lhsT_scale=theta_scales[:, first : first + P],
+                rhs=phi_codes[:, columns].bitcast(FP8X4),
+                rhs_scale=phi_scales[:, columns],
                 start=True,
                 stop=True,
             )
-            nc.scalar.mul(
-                out=result[:, piece * PIECE : (piece + 1) * PIECE], in_=acc[:], mul=1.0 / POINTS
-            )
-        nc.sync.dma_start(out=out_rows[columns, :], in_=result[:])
+            banks += 1
+            if banks % VECTOR_SHARE == 1:
+                nc.vector.tensor_scalar_mul(out=result[:, columns], in0=acc[:], scalar1=1.0 / POINTS)
+            else:
+                nc.scalar.mul(out=result[:, columns], in_=acc[:], mul=1.0 / POINTS)
+        nc.sync.dma_start(out=out_b[first : first + P, :], in_=result[:])
 
 
 def tile_sgcam_pa_kernel(tc, x, x_2, theta_w, theta_b, phi_w, phi_b, out):
     nc = tc.nc
     with ExitStack() as ctx:
         resident = ctx.enter_context(tc.tile_pool(name="resident", bufs=1))
-        stage = ctx.enter_context(tc.tile_pool(name="stage", bufs=3))
-        keep = ctx.enter_context(tc.tile_pool(name="keep", bufs=6))
+        stage = ctx.enter_context(tc.tile_pool(name="stage", bufs=4))
+        keep = ctx.enter_context(tc.tile_pool(name="keep", bufs=2))
         results = ctx.enter_context(tc.tile_pool(name="results", bufs=6))
         psum = ctx.enter_context(tc.psum_pool(name="psum", bufs=8))
+        ctx.enter_context(tc.manual_schedule())
 
         identity = resident.tile([P, P], F32)
         make_identity(nc, identity[:])
 
-        phi_raw, phi_bias = load_weights(nc, resident, phi_w, phi_b, "phi")
-        x_2_raw = [load_points(nc, resident, x_2[0], "x_2_raw0")]
-        theta_raw, theta_bias = load_weights(nc, resident, theta_w, theta_b, "theta")
-        x_raw = [load_points(nc, resident, x[0], "x_raw0")]
-        x_2_raw.append(load_points(nc, resident, x_2[1], "x_2_raw1"))
-        x_raw.append(load_points(nc, resident, x[1], "x_raw1"))
+        w_raw, bias, raw = {}, {}, {}
+        w_raw["phi"], bias["phi"] = load_weights(nc, resident, phi_w, phi_b, "phi")
+        raw["phi", 0] = load_points(nc, resident, x_2[0], "x_2_raw0")
+        w_raw["theta"], bias["theta"] = load_weights(nc, resident, theta_w, theta_b, "theta")
+        raw["theta", 0] = load_points(nc, resident, x[0], "x_raw0")
+        raw["phi", 1] = load_points(nc, resident, x_2[1], "x_2_raw1")
+        raw["theta", 1] = load_points(nc, resident, x[1], "x_raw1")
 
-        phi_weight = quantise_weights(nc, resident, psum, identity, phi_raw, "phi")
-        theta_weight = quantise_weights(nc, resident, psum, identity, theta_raw, "theta")
+        pieces = [(b, side, q) for b in range(BATCH) for side in ("phi", "theta") for q in range(PIECES)]
+        w_grouped = {}
+        weight = {}
+        quantised = {}
+        projected = {}
 
-        for b in range(BATCH):
-            phi = []
-            for piece in range(PIECES):
-                points = quantise_points(nc, stage, x_2_raw[b], piece)
-                phi.append(project(nc, stage, keep, psum, phi_weight, phi_bias, points))
-            for piece in range(PIECES):
-                points = quantise_points(nc, stage, x_raw[b], piece)
-                theta = project(nc, stage, keep, psum, theta_weight, theta_bias, points)
-                affinity(nc, results, psum, theta, phi, out[b, piece * PIECE : (piece + 1) * PIECE, :])
+        for turn in range(len(pieces) + LAG):
+            entering = turn < len(pieces)
+            leaving = turn >= LAG
+
+            side = pieces[min(turn + WEIGHT_LEAD, len(pieces) - 1)][1]
+            if side not in w_grouped:
+                w_grouped[side] = transpose_weights(nc, resident, psum, identity, w_raw[side], side)
+
+            if leaving:
+                projected_grouped = regroup_projection(nc, stage, projected[turn - LAG])
+            if entering:
+                b, side, q = pieces[turn]
+                points_grouped = stage.tile([P, PASSES, PIECE, PACK], BF16, align_bytes=64)
+                regroup_points(nc, raw[side, b], q, 0, points_grouped)
+            if leaving:
+                b, side, q = pieces[turn - LAG]
+                if q == 0:
+                    quantised[side, b] = (
+                        keep.tile([P, POINTS], U32, name="%s_codes" % side, align_bytes=64),
+                        keep.tile([P, POINTS], U8, name="%s_scales" % side, align_bytes=64),
+                    )
+                quantise_projection(nc, projected_grouped, quantised[side, b], q)
+            if entering:
+                b, side, q = pieces[turn]
+                regroup_points(nc, raw[side, b], q, 1, points_grouped)
+            if leaving:
+                b, side, q = pieces[turn - LAG]
+                if side == "theta":
+                    affinity(nc, results, psum, quantised["theta", b], quantised["phi", b], q, out[b])
+            if entering:
+                b, side, q = pieces[turn]
+                points = quantise_points(nc, stage, points_grouped)
+                if side not in weight:
+                    weight[side] = quantise_weights(nc, resident, w_grouped[side], side)
+                projected[turn] = project(nc, stage, psum, weight[side], bias[side], points)

@@ -18,11 +18,11 @@ K_PASS = P * PACK
 PASSES = CHANNELS // K_PASS
 WORD = 2
 BANK = 512
-PIECE = 256
+PIECE = 512
 PIECES = POINTS // PIECE
 LOAD = 512
 LAG = 2
-WEIGHT_LEAD = 2
+WEIGHT_LEAD = 1
 VECTOR_SHARE = 4
 
 FLOPS = 2 * BATCH * (2 * INNER * CHANNELS * POINTS + POINTS * POINTS * INNER)
@@ -166,7 +166,7 @@ def tile_sgcam_pa_kernel(tc, x, x_2, theta_w, theta_b, phi_w, phi_b, out):
     nc = tc.nc
     with ExitStack() as ctx:
         resident = ctx.enter_context(tc.tile_pool(name="resident", bufs=1))
-        stage = ctx.enter_context(tc.tile_pool(name="stage", bufs=4))
+        stage = ctx.enter_context(tc.tile_pool(name="stage", bufs=3))
         keep = ctx.enter_context(tc.tile_pool(name="keep", bufs=2))
         results = ctx.enter_context(tc.tile_pool(name="results", bufs=6))
         psum = ctx.enter_context(tc.psum_pool(name="psum", bufs=8))

@@ -23,7 +23,6 @@ PIECES = POINTS // PIECE
 LOAD = 512
 LAG = 2
 WEIGHT_LEAD = 1
-VECTOR_SHARE = 4
 
 FLOPS = 2 * BATCH * (2 * INNER * CHANNELS * POINTS + POINTS * POINTS * INNER)
 
@@ -140,7 +139,6 @@ def quantise_projection(nc, projected_grouped, quantised, q):
 def affinity(nc, pool, psum, theta, phi, q, out_b):
     theta_codes, theta_scales = theta
     phi_codes, phi_scales = phi
-    banks = 0
     for first in range(q * PIECE, (q + 1) * PIECE, P):
         result = pool.tile([P, POINTS], F32)
         for columns in [slice(n, n + BANK) for n in range(0, POINTS, BANK)]:
@@ -154,11 +152,7 @@ def affinity(nc, pool, psum, theta, phi, q, out_b):
                 start=True,
                 stop=True,
             )
-            banks += 1
-            if banks % VECTOR_SHARE == 1:
-                nc.vector.tensor_scalar_mul(out=result[:, columns], in0=acc[:], scalar1=1.0 / POINTS)
-            else:
-                nc.scalar.mul(out=result[:, columns], in_=acc[:], mul=1.0 / POINTS)
+            nc.scalar.mul(out=result[:, columns], in_=acc[:], mul=1.0 / POINTS)
         nc.sync.dma_start(out=out_b[first : first + P, :], in_=result[:])
 
 
@@ -197,12 +191,15 @@ def tile_sgcam_pa_kernel(tc, x, x_2, theta_w, theta_b, phi_w, phi_b, out):
             if side not in w_grouped:
                 w_grouped[side] = transpose_weights(nc, resident, psum, identity, w_raw[side], side)
 
-            if leaving:
-                projected_grouped = regroup_projection(nc, stage, projected[turn - LAG])
             if entering:
                 b, side, q = pieces[turn]
                 points_grouped = stage.tile([P, PASSES, PIECE, PACK], BF16, align_bytes=64)
-                regroup_points(nc, raw[side, b], q, 0, points_grouped)
+                for c in range(PASSES):
+                    regroup_points(nc, raw[side, b], q, c, points_grouped)
+            if leaving:
+                projected_grouped = regroup_projection(nc, stage, projected[turn - LAG])
+            if entering:
+                points = quantise_points(nc, stage, points_grouped)
             if leaving:
                 b, side, q = pieces[turn - LAG]
                 if q == 0:
@@ -211,16 +208,13 @@ def tile_sgcam_pa_kernel(tc, x, x_2, theta_w, theta_b, phi_w, phi_b, out):
                         keep.tile([P, POINTS], U8, name="%s_scales" % side, align_bytes=64),
                     )
                 quantise_projection(nc, projected_grouped, quantised[side, b], q)
+
             if entering:
                 b, side, q = pieces[turn]
-                regroup_points(nc, raw[side, b], q, 1, points_grouped)
+                if side not in weight:
+                    weight[side] = quantise_weights(nc, resident, w_grouped[side], side)
+                projected[turn] = project(nc, stage, psum, weight[side], bias[side], points)
             if leaving:
                 b, side, q = pieces[turn - LAG]
                 if side == "theta":
                     affinity(nc, results, psum, quantised["theta", b], quantised["phi", b], q, out[b])
-            if entering:
-                b, side, q = pieces[turn]
-                points = quantise_points(nc, stage, points_grouped)
-                if side not in weight:
-                    weight[side] = quantise_weights(nc, resident, w_grouped[side], side)
-                projected[turn] = project(nc, stage, psum, weight[side], bias[side], points)

@@ -49,10 +49,8 @@ def load_points(nc, pool, points, name):
 def load_weights(nc, pool, w, b, name):
     w_raw = pool.tile([P, PACK, CHANNELS], BF16, name="%s_raw" % name)
     nc.sync.dma_start(out=w_raw[:], in_=w.rearrange("(m t) k -> m t k", t=PACK))
-    bias_bf16 = pool.tile([P, PACK], BF16, name="%s_bias_bf16" % name)
-    nc.scalar.dma_start(out=bias_bf16[:], in_=b.rearrange("(m t) -> m t", t=PACK))
-    bias = pool.tile([P, PACK], F32, name="%s_bias" % name)
-    nc.vector.tensor_copy(out=bias[:], in_=bias_bf16[:])
+    bias = pool.tile([P, PACK], BF16, name="%s_bias" % name)
+    nc.scalar.dma_start(out=bias[:], in_=b.rearrange("(m t) -> m t", t=PACK))
     return w_raw, bias
 
 
@@ -119,10 +117,10 @@ def project(nc, pool, psum, weight, bias, points):
     return projected
 
 
-def regroup_projection(nc, pool, projected):
+def regroup_projection(copy, pool, projected):
     projected_grouped = pool.tile([P, PIECE, PACK], BF16, align_bytes=64)
     dst, src = side_by_side(projected[:], projected_grouped[:])
-    nc.vector.tensor_copy(out=dst, in_=src)
+    copy(out=dst, in_=src)
     return projected_grouped
 
 
@@ -182,6 +180,7 @@ def tile_sgcam_pa_kernel(tc, x, x_2, theta_w, theta_b, phi_w, phi_b, out):
         weight = {}
         quantised = {}
         projected = {}
+        projected_grouped = {}
 
         for turn in range(len(pieces) + LAG):
             entering = turn < len(pieces)
@@ -196,8 +195,10 @@ def tile_sgcam_pa_kernel(tc, x, x_2, theta_w, theta_b, phi_w, phi_b, out):
                 points_grouped = stage.tile([P, PASSES, PIECE, PACK], BF16, align_bytes=64)
                 for c in range(PASSES):
                     regroup_points(nc, raw[side, b], q, c, points_grouped)
-            if leaving:
-                projected_grouped = regroup_projection(nc, stage, projected[turn - LAG])
+            if leaving and turn - LAG not in projected_grouped:
+                projected_grouped[turn - LAG] = regroup_projection(
+                    nc.vector.tensor_copy, stage, projected[turn - LAG]
+                )
             if entering:
                 points = quantise_points(nc, stage, points_grouped)
             if leaving:
@@ -207,13 +208,15 @@ def tile_sgcam_pa_kernel(tc, x, x_2, theta_w, theta_b, phi_w, phi_b, out):
                         keep.tile([P, POINTS], U32, name="%s_codes" % side, align_bytes=64),
                         keep.tile([P, POINTS], U8, name="%s_scales" % side, align_bytes=64),
                     )
-                quantise_projection(nc, projected_grouped, quantised[side, b], q)
+                quantise_projection(nc, projected_grouped[turn - LAG], quantised[side, b], q)
 
             if entering:
                 b, side, q = pieces[turn]
                 if side not in weight:
                     weight[side] = quantise_weights(nc, resident, w_grouped[side], side)
                 projected[turn] = project(nc, stage, psum, weight[side], bias[side], points)
+                if (b, side) == (0, "phi"):
+                    projected_grouped[turn] = regroup_projection(nc.scalar.copy, stage, projected[turn])
             if leaving:
                 b, side, q = pieces[turn - LAG]
                 if side == "theta":

@@ -20,7 +20,6 @@ WORD = 2
 BANK = 512
 PIECE = 512
 PIECES = POINTS // PIECE
-LOAD = 512
 LAG = 2
 WEIGHT_LEAD = 1
 
@@ -35,14 +34,12 @@ def side_by_side(rows_apart, together):
 
 
 def load_points(nc, pool, points, name):
-    raw = pool.tile([P, PASSES, PACK, POINTS], BF16, name=name)
-    for first in range(0, POINTS, LOAD):
+    raw = []
+    for q in range(PIECES):
+        raw.append(pool.tile([P, PASSES, PACK, PIECE], BF16, name="%s_%d" % (name, q)))
         for c in range(PASSES):
-            rows = points[c * K_PASS : (c + 1) * K_PASS, first : first + LOAD]
-            nc.sync.dma_start(
-                out=raw[:, c, :, first : first + LOAD],
-                in_=rows.rearrange("(p j) n -> p j n", j=PACK),
-            )
+            rows = points[c * K_PASS : (c + 1) * K_PASS, q * PIECE : (q + 1) * PIECE]
+            nc.sync.dma_start(out=raw[q][:, c], in_=rows.rearrange("(p j) n -> p j n", j=PACK))
     return raw
 
 
@@ -78,8 +75,8 @@ def quantise_weights(nc, pool, grouped, name):
     return codes, scales
 
 
-def regroup_points(nc, raw, q, c, points_grouped):
-    dst, src = side_by_side(raw[:, c, :, q * PIECE : (q + 1) * PIECE], points_grouped[:, c])
+def regroup_points(nc, raw, c, points_grouped):
+    dst, src = side_by_side(raw[:, c], points_grouped[:, c])
     nc.vector.tensor_copy(out=dst, in_=src)
 
 
@@ -117,10 +114,10 @@ def project(nc, pool, psum, weight, bias, points):
     return projected
 
 
-def regroup_projection(copy, pool, projected):
+def regroup_projection(nc, pool, projected):
     projected_grouped = pool.tile([P, PIECE, PACK], BF16, align_bytes=64)
     dst, src = side_by_side(projected[:], projected_grouped[:])
-    copy(out=dst, in_=src)
+    nc.vector.tensor_copy(out=dst, in_=src)
     return projected_grouped
 
 
@@ -180,7 +177,6 @@ def tile_sgcam_pa_kernel(tc, x, x_2, theta_w, theta_b, phi_w, phi_b, out):
         weight = {}
         quantised = {}
         projected = {}
-        projected_grouped = {}
 
         for turn in range(len(pieces) + LAG):
             entering = turn < len(pieces)
@@ -194,11 +190,9 @@ def tile_sgcam_pa_kernel(tc, x, x_2, theta_w, theta_b, phi_w, phi_b, out):
                 b, side, q = pieces[turn]
                 points_grouped = stage.tile([P, PASSES, PIECE, PACK], BF16, align_bytes=64)
                 for c in range(PASSES):
-                    regroup_points(nc, raw[side, b], q, c, points_grouped)
-            if leaving and turn - LAG not in projected_grouped:
-                projected_grouped[turn - LAG] = regroup_projection(
-                    nc.vector.tensor_copy, stage, projected[turn - LAG]
-                )
+                    regroup_points(nc, raw[side, b][q], c, points_grouped)
+            if leaving:
+                projected_grouped = regroup_projection(nc, stage, projected[turn - LAG])
             if entering:
                 points = quantise_points(nc, stage, points_grouped)
             if leaving:
@@ -208,15 +202,13 @@ def tile_sgcam_pa_kernel(tc, x, x_2, theta_w, theta_b, phi_w, phi_b, out):
                         keep.tile([P, POINTS], U32, name="%s_codes" % side, align_bytes=64),
                         keep.tile([P, POINTS], U8, name="%s_scales" % side, align_bytes=64),
                     )
-                quantise_projection(nc, projected_grouped[turn - LAG], quantised[side, b], q)
+                quantise_projection(nc, projected_grouped, quantised[side, b], q)
 
             if entering:
                 b, side, q = pieces[turn]
                 if side not in weight:
                     weight[side] = quantise_weights(nc, resident, w_grouped[side], side)
                 projected[turn] = project(nc, stage, psum, weight[side], bias[side], points)
-                if (b, side) == (0, "phi"):
-                    projected_grouped[turn] = regroup_projection(nc.scalar.copy, stage, projected[turn])
             if leaving:
                 b, side, q = pieces[turn - LAG]
                 if side == "theta":

@@ -8,7 +8,6 @@ BF16 = mybir.dt.bfloat16
 F32 = mybir.dt.float32
 U32 = mybir.dt.uint32
 U8 = mybir.dt.uint8
-IDENTITY = mybir.ActivationFunctionType.Identity
 
 BATCH, CHANNELS, INNER, POINTS = 2, 1024, 512, 1024
 
@@ -18,10 +17,8 @@ K_PASS = P * PACK
 PASSES = CHANNELS // K_PASS
 WORD = 2
 BANK = 512
-PIECE = 512
-PIECES = POINTS // PIECE
-LAG = 2
-WEIGHT_LEAD = 1
+
+CONFIG = {"pieces":[[0,"phi",0,512],[0,"theta",0,512],[0,"phi",512,512],[0,"theta",512,512],[1,"phi",0,512],[1,"theta",0,512],[1,"phi",512,256],[1,"theta",512,256],[1,"phi",768,256],[1,"theta",768,256]],"loads":[["x",0,0],["x",0,1],["W","phi"],["x",1,0],["x",1,1],["W","theta"],["x",2,0],["x",2,1],["x",3,0],["x",3,1],["x",4,0],["x",4,1],["x",5,0],["x",5,1],["x",6,0],["x",6,1],["x",7,0],["x",7,1],["x",8,0],["x",8,1],["x",9,0],["x",9,1]],"g":[0,256,384,384,384,384,192,192,192,192],"s":[256,512,512,512,512,512,256,256,256,256],"qa":[0,0,0,1,1,1,1,1,1,2,2,4],"qk":[0,0,1,1,1,1,1,1,1,1,1,1],"qb":[0,0,0,0,1,1,1,1,1,2,4,9],"ea":["S","S","S","S","S","S","S","S","S","S","SV","SV"],"ek":["S","S","S","S","S","S","S","S","S","S","SV","SV"],"eb":["S","S","S","S","S","S","S","S","S","S","SV","SV"],"we":["SS","SS","SS","SS"],"mut":["g","s","qa","qk","qb","ea","ek","eb","loads","we"]}
 
 FLOPS = 2 * BATCH * (2 * INNER * CHANNELS * POINTS + POINTS * POINTS * INNER)
 
@@ -33,97 +30,57 @@ def side_by_side(rows_apart, together):
     )
 
 
-def load_points(nc, pool, points, name):
-    raw = []
-    for q in range(PIECES):
-        raw.append(pool.tile([P, PASSES, PACK, PIECE], BF16, name="%s_%d" % (name, q)))
-        for c in range(PASSES):
-            rows = points[c * K_PASS : (c + 1) * K_PASS, q * PIECE : (q + 1) * PIECE]
-            nc.sync.dma_start(out=raw[q][:, c], in_=rows.rearrange("(p j) n -> p j n", j=PACK))
-    return raw
+def load_points(nc, raw, points, c, first, width):
+    rows = points[c * K_PASS : (c + 1) * K_PASS, first : first + width]
+    nc.sync.dma_start(out=raw[:, c], in_=rows.rearrange("(p j) n -> p j n", j=PACK))
 
 
-def load_weights(nc, pool, w, b, name):
-    w_raw = pool.tile([P, PACK, CHANNELS], BF16, name="%s_raw" % name)
-    nc.sync.dma_start(out=w_raw[:], in_=w.rearrange("(m t) k -> m t k", t=PACK))
-    bias = pool.tile([P, PACK], BF16, name="%s_bias" % name)
-    nc.scalar.dma_start(out=bias[:], in_=b.rearrange("(m t) -> m t", t=PACK))
-    return w_raw, bias
-
-
-def transpose_weights(nc, pool, psum, identity, w_raw, name):
+def transpose_weights(nc, psum, identity, w_raw, grouped, c, eng):
     words = w_raw[:].bitcast(F32).rearrange("m t (c p u) -> m t c u p", c=PASSES, u=PACK // WORD)
-    grouped = pool.tile([P, PASSES, PACK, P, PACK], BF16, name="%s_grouped" % name, align_bytes=64)
     grouped_words = grouped[:].bitcast(F32)
-    for t in range(PACK):
-        flipped = psum.tile([P, PASSES, PACK // WORD, P], F32, tag="bank")
-        for c in range(PASSES):
+    for t2 in range(PACK // 2):
+        flipped = psum.tile([P, 2, PACK // WORD, P], F32, tag="bank", bufs=4, name="flipped")
+        for t in range(2):
             for u in range(PACK // WORD):
-                nc.tensor.transpose(flipped[:, c, u, :], words[:, t, c, u, :], identity[:])
-        nc.scalar.copy(out=grouped_words[:, :, t], in_=flipped[:].rearrange("p c u m -> p c m u"))
-    return grouped
+                nc.tensor.transpose(flipped[:, t, u, :], words[:, 2 * t2 + t, c, u, :], identity[:])
+        out = grouped_words[:, c, 2 * t2 : 2 * t2 + 2]
+        in_ = flipped[:].rearrange("p t u m -> p t m u")
+        if eng[t2] == "V":
+            nc.vector.tensor_copy(out=out, in_=in_)
+        else:
+            nc.scalar.copy(out=out, in_=in_)
 
 
-def quantise_weights(nc, pool, grouped, name):
-    codes = pool.tile([P, PASSES, INNER], U32, name="%s_w_codes" % name, align_bytes=64)
-    scales = pool.tile([P, PASSES, INNER], U8, name="%s_w_scales" % name, align_bytes=64)
+def quantise_weights(nc, grouped, c, weight):
+    codes, scales = weight
     nc.vector.quantize_mx(
-        out=codes[:].rearrange("p c n -> p (c n)").bitcast(FP8X4),
-        scales=scales[:].rearrange("p c n -> p (c n)"),
-        in_=grouped[:].rearrange("p c t m j -> p (c t m j)"),
+        out=codes[:, c].bitcast(FP8X4),
+        scales=scales[:, c],
+        in_=grouped[:, c].rearrange("p t m j -> p (t m j)"),
     )
-    return codes, scales
 
 
-def regroup_points(nc, raw, c, points_grouped):
-    dst, src = side_by_side(raw[:, c], points_grouped[:, c])
-    nc.vector.tensor_copy(out=dst, in_=src)
+def regroup(nc, engine, apart, together):
+    dst, src = side_by_side(apart, together)
+    if engine == "V":
+        nc.vector.tensor_copy(out=dst, in_=src)
+    elif engine == "G":
+        nc.gpsimd.tensor_scalar(out=dst, in0=src, scalar1=1.0, scalar2=0.0, op0=mybir.AluOpType.mult, op1=mybir.AluOpType.add)
+    else:
+        nc.scalar.copy(out=dst, in_=src)
 
 
-def quantise_points(nc, pool, points_grouped):
-    points_codes = pool.tile([P, PASSES, PIECE], U32, align_bytes=64)
-    points_scales = pool.tile([P, PASSES, PIECE], U8, align_bytes=64)
+def quantise_points(nc, points_grouped, c, points):
+    codes, scales = points
     nc.vector.quantize_mx(
-        out=points_codes[:].rearrange("p c n -> p (c n)").bitcast(FP8X4),
-        scales=points_scales[:].rearrange("p c n -> p (c n)"),
-        in_=points_grouped[:].rearrange("p c n j -> p (c n j)"),
+        out=codes[:, c, :].bitcast(FP8X4),
+        scales=scales[:, c, :],
+        in_=points_grouped[:, c].rearrange("p n j -> p (n j)"),
     )
-    return points_codes, points_scales
 
 
-def project(nc, pool, psum, weight, bias, points):
-    w_codes, w_scales = weight
-    points_codes, points_scales = points
-    projected = pool.tile([P, PACK, PIECE], BF16)
-    for t in range(PACK):
-        columns = slice(t * P, (t + 1) * P)
-        acc = psum.tile([P, PIECE], F32, tag="bank")
-        for c in range(PASSES):
-            nc.tensor.matmul_mx(
-                out=acc[:],
-                lhsT=w_codes[:, c, columns].bitcast(FP8X4),
-                lhsT_scale=w_scales[:, c, columns],
-                rhs=points_codes[:, c, :].bitcast(FP8X4),
-                rhs_scale=points_scales[:, c, :],
-                start=(c == 0),
-                stop=(c == PASSES - 1),
-            )
-        nc.scalar.activation(
-            out=projected[:, t, :], in_=acc[:], func=IDENTITY, bias=bias[:, t : t + 1], scale=1.0
-        )
-    return projected
-
-
-def regroup_projection(nc, pool, projected):
-    projected_grouped = pool.tile([P, PIECE, PACK], BF16, align_bytes=64)
-    dst, src = side_by_side(projected[:], projected_grouped[:])
-    nc.vector.tensor_copy(out=dst, in_=src)
-    return projected_grouped
-
-
-def quantise_projection(nc, projected_grouped, quantised, q):
+def quantise_projection(nc, projected_grouped, quantised, columns):
     codes, scales = quantised
-    columns = slice(q * PIECE, (q + 1) * PIECE)
     nc.vector.quantize_mx(
         out=codes[:, columns].bitcast(FP8X4),
         scales=scales[:, columns],
@@ -131,85 +88,231 @@ def quantise_projection(nc, projected_grouped, quantised, q):
     )
 
 
-def affinity(nc, pool, psum, theta, phi, q, out_b):
+def affinity(nc, pool, psum, theta, phi, row, column, width, out_b, engine):
     theta_codes, theta_scales = theta
     phi_codes, phi_scales = phi
-    for first in range(q * PIECE, (q + 1) * PIECE, P):
-        result = pool.tile([P, POINTS], F32)
-        for columns in [slice(n, n + BANK) for n in range(0, POINTS, BANK)]:
-            acc = psum.tile([P, BANK], F32, tag="bank")
-            nc.tensor.matmul_mx(
-                out=acc[:],
-                lhsT=theta_codes[:, first : first + P].bitcast(FP8X4),
-                lhsT_scale=theta_scales[:, first : first + P],
-                rhs=phi_codes[:, columns].bitcast(FP8X4),
-                rhs_scale=phi_scales[:, columns],
-                start=True,
-                stop=True,
-            )
-            nc.scalar.mul(out=result[:, columns], in_=acc[:], mul=1.0 / POINTS)
-        nc.sync.dma_start(out=out_b[first : first + P, :], in_=result[:])
+    rows, columns = slice(row, row + P), slice(column, column + width)
+    acc = psum.tile([P, width], F32, tag="bank", bufs=4, name="acc_affinity")
+    nc.tensor.matmul_mx(
+        out=acc[:],
+        lhsT=theta_codes[:, rows].bitcast(FP8X4),
+        lhsT_scale=theta_scales[:, rows],
+        rhs=phi_codes[:, columns].bitcast(FP8X4),
+        rhs_scale=phi_scales[:, columns],
+        start=True,
+        stop=True,
+    )
+    result = pool.tile([P, width], F32, name="result_%d" % width)
+    if engine == "V":
+        nc.vector.tensor_scalar_mul(out=result[:], in0=acc[:], scalar1=1.0 / POINTS)
+    else:
+        nc.scalar.mul(out=result[:], in_=acc[:], mul=1.0 / POINTS)
+    nc.sync.dma_start(out=out_b[rows, columns], in_=result[:])
 
 
 def tile_sgcam_pa_kernel(tc, x, x_2, theta_w, theta_b, phi_w, phi_b, out):
     nc = tc.nc
     with ExitStack() as ctx:
         resident = ctx.enter_context(tc.tile_pool(name="resident", bufs=1))
-        stage = ctx.enter_context(tc.tile_pool(name="stage", bufs=3))
+        stage = ctx.enter_context(tc.tile_pool(name="stage", bufs=2))
         keep = ctx.enter_context(tc.tile_pool(name="keep", bufs=2))
-        results = ctx.enter_context(tc.tile_pool(name="results", bufs=6))
-        psum = ctx.enter_context(tc.psum_pool(name="psum", bufs=8))
+        results = ctx.enter_context(tc.tile_pool(name="results", bufs=12))
+        psum = ctx.enter_context(tc.psum_pool(name="psum", bufs=1))
         ctx.enter_context(tc.manual_schedule())
 
         identity = resident.tile([P, P], F32)
         make_identity(nc, identity[:])
 
-        w_raw, bias, raw = {}, {}, {}
-        w_raw["phi"], bias["phi"] = load_weights(nc, resident, phi_w, phi_b, "phi")
-        raw["phi", 0] = load_points(nc, resident, x_2[0], "x_2_raw0")
-        w_raw["theta"], bias["theta"] = load_weights(nc, resident, theta_w, theta_b, "theta")
-        raw["theta", 0] = load_points(nc, resident, x[0], "x_raw0")
-        raw["phi", 1] = load_points(nc, resident, x_2[1], "x_2_raw1")
-        raw["theta", 1] = load_points(nc, resident, x[1], "x_raw1")
+        inputs = {"phi": (x_2, phi_w, phi_b), "theta": (x, theta_w, theta_b)}
+        pieces = CONFIG["pieces"]
+        raw = {}
+        for i, (b, side, first, width) in enumerate(pieces):
+            tile = resident.tile([P, PASSES, PACK, width], BF16, name="raw_%d" % i)
+            raw[i] = tile
+        w_raw, bias, w_grouped, weight = {}, {}, {}, {}
+        for side in ("phi", "theta"):
+            w_raw_tile = resident.tile([P, PACK, CHANNELS], BF16, name="%s_w_raw" % side)
+            bias_tile = resident.tile([P, PACK], BF16, name="%s_bias" % side)
+            grouped_tile = resident.tile([P, PASSES, PACK, P, PACK], BF16, name="%s_w_grouped" % side, align_bytes=64)
+            codes = resident.tile([P, PASSES, INNER], U32, name="%s_w_codes" % side, align_bytes=64)
+            scales = resident.tile([P, PASSES, INNER], U8, name="%s_w_scales" % side, align_bytes=64)
+            w_raw[side], bias[side], w_grouped[side], weight[side] = w_raw_tile, bias_tile, grouped_tile, (codes, scales)
+            nc.scalar.dma_start(out=bias_tile[:], in_=inputs[side][2].rearrange("(m t) -> m t", t=PACK))
 
-        pieces = [(b, side, q) for b in range(BATCH) for side in ("phi", "theta") for q in range(PIECES)]
-        w_grouped = {}
-        weight = {}
-        quantised = {}
-        projected = {}
+        for step in CONFIG["loads"]:
+            if step[0] == "w":
+                side, half = step[1], step[2]
+                ks = slice(half * K_PASS, (half + 1) * K_PASS)
+                nc.sync.dma_start(
+                    out=w_raw[side][:, :, ks],
+                    in_=inputs[side][1].rearrange("(m t) k -> m t k", t=PACK)[:, :, ks],
+                )
+            elif step[0] == "W":
+                side = step[1]
+                nc.sync.dma_start(out=w_raw[side][:], in_=inputs[side][1].rearrange("(m t) k -> m t k", t=PACK))
+            else:
+                i, c = step[1], step[2]
+                b, side, first, width = pieces[i]
+                load_points(nc, raw[i], inputs[side][0][b], c, first, width)
 
-        for turn in range(len(pieces) + LAG):
-            entering = turn < len(pieces)
-            leaving = turn >= LAG
+        quantised, projected, grouped, points = {}, {}, {}, {}
+        jobs = []
 
-            side = pieces[min(turn + WEIGHT_LEAD, len(pieces) - 1)][1]
-            if side not in w_grouped:
-                w_grouped[side] = transpose_weights(nc, resident, psum, identity, w_raw[side], side)
+        def get_grouped(i):
+            if i not in grouped:
+                width = pieces[i][3]
+                tile = stage.tile([P, PASSES, width, PACK], BF16, name="points_grouped_%d" % width, align_bytes=64)
+                grouped[i] = tile
+            return grouped[i]
 
-            if entering:
-                b, side, q = pieces[turn]
-                points_grouped = stage.tile([P, PASSES, PIECE, PACK], BF16, align_bytes=64)
+        def x1(i, c, engine, lo=0, hi=None):
+            hi = pieces[i][3] if hi is None else hi
+            if hi > lo:
+                regroup(nc, engine, raw[i][:, c, :, lo:hi], get_grouped(i)[:, c, lo:hi])
+
+        def q(i):
+            width = pieces[i][3]
+            codes = stage.tile([P, PASSES, width], U32, name="points_codes_%d" % width, align_bytes=64)
+            scales = stage.tile([P, PASSES, width], U8, name="points_scales_%d" % width, align_bytes=64)
+            points[i] = (codes, scales)
+            nc.vector.quantize_mx(
+                out=codes[:].rearrange("p c n -> p (c n)").bitcast(FP8X4),
+                scales=scales[:].rearrange("p c n -> p (c n)"),
+                in_=grouped[i][:].rearrange("p c n j -> p (c n j)"),
+            )
+
+        pg = {}
+
+        def banks(i):
+            return pieces[i][3] // P
+
+        def pj(i, k):
+            b, side, first, width = pieces[i]
+            w_codes, w_scales = weight[side]
+            codes, scales = points[i]
+            acc = psum.tile([P, PACK, P], F32, tag="projection", bufs=4, name="acc_projection")
+            projected[i, k] = acc
+            cols = slice(k * P, (k + 1) * P)
+            for t in range(PACK):
                 for c in range(PASSES):
-                    regroup_points(nc, raw[side, b][q], c, points_grouped)
-            if leaving:
-                projected_grouped = regroup_projection(nc, stage, projected[turn - LAG])
-            if entering:
-                points = quantise_points(nc, stage, points_grouped)
-            if leaving:
-                b, side, q = pieces[turn - LAG]
-                if q == 0:
-                    quantised[side, b] = (
-                        keep.tile([P, POINTS], U32, name="%s_codes" % side, align_bytes=64),
-                        keep.tile([P, POINTS], U8, name="%s_scales" % side, align_bytes=64),
+                    nc.tensor.matmul_mx(
+                        out=acc[:, t, :],
+                        lhsT=w_codes[:, c, t * P : (t + 1) * P].bitcast(FP8X4),
+                        lhsT_scale=w_scales[:, c, t * P : (t + 1) * P],
+                        rhs=codes[:, c, cols].bitcast(FP8X4),
+                        rhs_scale=scales[:, c, cols],
+                        start=(c == 0),
+                        stop=(c == PASSES - 1),
                     )
-                quantise_projection(nc, projected_grouped, quantised[side, b], q)
 
-            if entering:
-                b, side, q = pieces[turn]
-                if side not in weight:
-                    weight[side] = quantise_weights(nc, resident, w_grouped[side], side)
-                projected[turn] = project(nc, stage, psum, weight[side], bias[side], points)
-            if leaving:
-                b, side, q = pieces[turn - LAG]
-                if side == "theta":
-                    affinity(nc, results, psum, quantised["theta", b], quantised["phi", b], q, out[b])
+        def pjd(i, k):
+            b, side, first, width = pieces[i]
+            if k == 0:
+                tile = stage.tile([P, width, PACK], BF16, name="projected_grouped_%d" % width, align_bytes=64)
+                pg[i] = tile
+            nc.vector.tensor_tensor(
+                out=pg[i][:, k * P : (k + 1) * P, :],
+                in0=projected[i, k][:].rearrange("p t n -> p n t"),
+                in1=bias[side][:].unsqueeze(1).to_broadcast([P, P, PACK]),
+                op=mybir.AluOpType.add,
+            )
+
+        done = {}
+
+        def qp(i):
+            b, side, first, width = pieces[i]
+            if (side, b) not in quantised:
+                codes = keep.tile([P, POINTS], U32, name="%s_codes" % side, align_bytes=64)
+                scales = keep.tile([P, POINTS], U8, name="%s_scales" % side, align_bytes=64)
+                quantised[side, b] = (codes, scales)
+                done[side, b] = []
+            quantise_projection(nc, pg[i], quantised[side, b], slice(first, first + width))
+            done[side, b].append((first, width))
+            other = "theta" if side == "phi" else "phi"
+            ranges = sorted(done.get((other, b), []))
+            merged = []
+            for f, w in ranges:
+                if merged and merged[-1][1] == f and f % BANK:
+                    merged[-1] = (merged[-1][0], f + w)
+                else:
+                    merged.append((f, f + w))
+            if side == "phi":
+                for f, e in merged:
+                    for row in range(f, e, P):
+                        jobs.append((b, row, first, width))
+            else:
+                for row in range(first, first + width, P):
+                    for f, e in merged:
+                        jobs.append((b, row, f, e - f))
+
+        def jobs_run(n, engines):
+            for k in range(min(n, len(jobs))):
+                b, row, column, width = jobs[0]
+                jobs.remove(jobs[0])
+                affinity(nc, results, psum, quantised["theta", b], quantised["phi", b], row, column, width, out[b], engines[k % len(engines)])
+
+        def wt(side, c, eng="SS"):
+            transpose_weights(nc, psum, identity, w_raw[side], w_grouped[side], c, eng)
+
+        def wq(side):
+            codes, scales = weight[side]
+            nc.vector.quantize_mx(
+                out=codes[:].rearrange("p c n -> p (c n)").bitcast(FP8X4),
+                scales=scales[:].rearrange("p c n -> p (c n)"),
+                in_=w_grouped[side][:].rearrange("p c t m j -> p (c t m j)"),
+            )
+
+
+        CFG = CONFIG
+        gs, ss, qa, qk, qb, ea, ek, eb = [CFG[k] for k in ("g", "s", "qa", "qk", "qb", "ea", "ek", "eb")]
+        n = len(pieces)
+
+        def xg(i):
+            x1(i, 0, "G", 0, gs[i])
+
+        def xs(i):
+            w = pieces[i][3]
+            x1(i, 1, "S", w - ss[i], w)
+
+        def xv(i):
+            w = pieces[i][3]
+            x1(i, 0, "V", gs[i], w)
+            x1(i, 1, "V", 0, w - ss[i])
+
+        xg(0)
+        xs(0)
+        xv(0)
+        wt("phi", 0, CFG["we"][0])
+        wt("phi", 1, CFG["we"][1])
+        xg(1)
+        xs(1)
+        q(0)
+        xv(1)
+        wq("phi")
+        wt("theta", 0, CFG["we"][2])
+        wt("theta", 1, CFG["we"][3])
+        for k in range(banks(0)):
+            pj(0, k)
+        xg(2)
+        xs(2)
+        for i in range(1, n + 2):
+            if i < n:
+                q(i)
+            if i == 1:
+                wq("theta")
+            jobs_run(qa[i], ea[i])
+            if i + 2 < n and i > 0:
+                xg(i + 2)
+            for k in range(4):
+                if i - 1 < n and k < banks(i - 1):
+                    pjd(i - 1, k)
+                if i < n and k < banks(i):
+                    pj(i, k)
+                jobs_run(qk[i], ek[i])
+            if i + 2 < n and i > 0:
+                xs(i + 2)
+            if i + 1 < n:
+                xv(i + 1)
+            if i - 1 < n:
+                qp(i - 1)
+            jobs_run(qb[i], eb[i])

@@ -8,6 +8,8 @@ BF16 = mybir.dt.bfloat16
 F32 = mybir.dt.float32
 U32 = mybir.dt.uint32
 U8 = mybir.dt.uint8
+ADD = mybir.AluOpType.add
+MULT = mybir.AluOpType.mult
 
 BATCH, CHANNELS, INNER, POINTS = 2, 1024, 512, 1024
 
@@ -18,301 +20,277 @@ PASSES = CHANNELS // K_PASS
 WORD = 2
 BANK = 512
 
-CONFIG = {"pieces":[[0,"phi",0,512],[0,"theta",0,512],[0,"phi",512,512],[0,"theta",512,512],[1,"phi",0,512],[1,"theta",0,512],[1,"phi",512,256],[1,"theta",512,256],[1,"phi",768,256],[1,"theta",768,256]],"loads":[["x",0,0],["x",0,1],["W","phi"],["x",1,0],["x",1,1],["W","theta"],["x",2,0],["x",2,1],["x",3,0],["x",3,1],["x",4,0],["x",4,1],["x",5,0],["x",5,1],["x",6,0],["x",6,1],["x",7,0],["x",7,1],["x",8,0],["x",8,1],["x",9,0],["x",9,1]],"g":[0,256,384,384,384,384,192,192,192,192],"s":[256,512,512,512,512,512,256,256,256,256],"qa":[0,0,0,1,1,1,1,1,1,2,2,4],"qk":[0,0,1,1,1,1,1,1,1,1,1,1],"qb":[0,0,0,0,1,1,1,1,1,2,4,9],"ea":["S","S","S","S","S","S","S","S","S","S","SV","SV"],"ek":["S","S","S","S","S","S","S","S","S","S","SV","SV"],"eb":["S","S","S","S","S","S","S","S","S","S","SV","SV"],"we":["SS","SS","SS","SS"],"mut":["g","s","qa","qk","qb","ea","ek","eb","loads","we"]}
-
 FLOPS = 2 * BATCH * (2 * INNER * CHANNELS * POINTS + POINTS * POINTS * INNER)
+
+PIECES = [
+    (0, "phi", 0, 512),
+    (0, "theta", 0, 512),
+    (0, "phi", 512, 512),
+    (0, "theta", 512, 512),
+    (1, "phi", 0, 512),
+    (1, "theta", 0, 512),
+    (1, "phi", 512, 512),
+    (1, "theta", 512, 256),
+    (1, "theta", 768, 256),
+]
+LAST = len(PIECES)
+HEAD = 2
+LAG_UNTIL = 7
+
+
+def banks(i):
+    return PIECES[i][3] // P
 
 
 def side_by_side(rows_apart, together):
-    return (
-        together.rearrange("p (g i) j -> p g j i", i=4),
-        rows_apart.rearrange("p j (g i) -> p g j i", i=4),
-    )
+    return {
+        "out": together.rearrange("p (g i) j -> p g j i", i=4),
+        "in_": rows_apart.rearrange("p j (g i) -> p g j i", i=4),
+    }
 
 
-def load_points(nc, raw, points, c, first, width):
-    rows = points[c * K_PASS : (c + 1) * K_PASS, first : first + width]
-    nc.sync.dma_start(out=raw[:, c], in_=rows.rearrange("(p j) n -> p j n", j=PACK))
-
-
-def transpose_weights(nc, psum, identity, w_raw, grouped, c, eng):
+def transpose_weights(nc, psum, identity, w_raw, grouped, engines):
     words = w_raw[:].bitcast(F32).rearrange("m t (c p u) -> m t c u p", c=PASSES, u=PACK // WORD)
     grouped_words = grouped[:].bitcast(F32)
-    for t2 in range(PACK // 2):
-        flipped = psum.tile([P, 2, PACK // WORD, P], F32, tag="bank", bufs=4, name="flipped")
-        for t in range(2):
-            for u in range(PACK // WORD):
-                nc.tensor.transpose(flipped[:, t, u, :], words[:, 2 * t2 + t, c, u, :], identity[:])
-        out = grouped_words[:, c, 2 * t2 : 2 * t2 + 2]
-        in_ = flipped[:].rearrange("p t u m -> p t m u")
-        if eng[t2] == "V":
-            nc.vector.tensor_copy(out=out, in_=in_)
-        else:
-            nc.scalar.copy(out=out, in_=in_)
+    for c in range(PASSES):
+        for first in range(0, PACK, 2):
+            flipped = psum.tile([P, 2, PACK // WORD, P], F32, tag="product", name="flipped")
+            for t in range(2):
+                for u in range(PACK // WORD):
+                    nc.tensor.transpose(flipped[:, t, u, :], words[:, first + t, c, u, :], identity[:])
+            out = grouped_words[:, c, first : first + 2]
+            in_ = flipped[:].rearrange("p t u m -> p t m u")
+            if engines[first // 2] == "vector":
+                nc.vector.tensor_copy(out=out, in_=in_)
+            else:
+                nc.scalar.copy(out=out, in_=in_)
 
 
-def quantise_weights(nc, grouped, c, weight):
-    codes, scales = weight
+def quantise(nc, codes, scales, values):
     nc.vector.quantize_mx(
-        out=codes[:, c].bitcast(FP8X4),
-        scales=scales[:, c],
-        in_=grouped[:, c].rearrange("p t m j -> p (t m j)"),
+        out=codes.bitcast(FP8X4), scales=scales, in_=values.rearrange("p n j -> p (n j)")
     )
-
-
-def regroup(nc, engine, apart, together):
-    dst, src = side_by_side(apart, together)
-    if engine == "V":
-        nc.vector.tensor_copy(out=dst, in_=src)
-    elif engine == "G":
-        nc.gpsimd.tensor_scalar(out=dst, in0=src, scalar1=1.0, scalar2=0.0, op0=mybir.AluOpType.mult, op1=mybir.AluOpType.add)
-    else:
-        nc.scalar.copy(out=dst, in_=src)
-
-
-def quantise_points(nc, points_grouped, c, points):
-    codes, scales = points
-    nc.vector.quantize_mx(
-        out=codes[:, c, :].bitcast(FP8X4),
-        scales=scales[:, c, :],
-        in_=points_grouped[:, c].rearrange("p n j -> p (n j)"),
-    )
-
-
-def quantise_projection(nc, projected_grouped, quantised, columns):
-    codes, scales = quantised
-    nc.vector.quantize_mx(
-        out=codes[:, columns].bitcast(FP8X4),
-        scales=scales[:, columns],
-        in_=projected_grouped[:].rearrange("p n j -> p (n j)"),
-    )
-
-
-def affinity(nc, pool, psum, theta, phi, row, column, width, out_b, engine):
-    theta_codes, theta_scales = theta
-    phi_codes, phi_scales = phi
-    rows, columns = slice(row, row + P), slice(column, column + width)
-    acc = psum.tile([P, width], F32, tag="bank", bufs=4, name="acc_affinity")
-    nc.tensor.matmul_mx(
-        out=acc[:],
-        lhsT=theta_codes[:, rows].bitcast(FP8X4),
-        lhsT_scale=theta_scales[:, rows],
-        rhs=phi_codes[:, columns].bitcast(FP8X4),
-        rhs_scale=phi_scales[:, columns],
-        start=True,
-        stop=True,
-    )
-    result = pool.tile([P, width], F32, name="result_%d" % width)
-    if engine == "V":
-        nc.vector.tensor_scalar_mul(out=result[:], in0=acc[:], scalar1=1.0 / POINTS)
-    else:
-        nc.scalar.mul(out=result[:], in_=acc[:], mul=1.0 / POINTS)
-    nc.sync.dma_start(out=out_b[rows, columns], in_=result[:])
 
 
 def tile_sgcam_pa_kernel(tc, x, x_2, theta_w, theta_b, phi_w, phi_b, out):
     nc = tc.nc
+    inputs = {"phi": (x_2, phi_w, phi_b), "theta": (x, theta_w, theta_b)}
     with ExitStack() as ctx:
         resident = ctx.enter_context(tc.tile_pool(name="resident", bufs=1))
         stage = ctx.enter_context(tc.tile_pool(name="stage", bufs=2))
-        keep = ctx.enter_context(tc.tile_pool(name="keep", bufs=2))
-        results = ctx.enter_context(tc.tile_pool(name="results", bufs=12))
-        psum = ctx.enter_context(tc.psum_pool(name="psum", bufs=1))
+        results = ctx.enter_context(tc.tile_pool(name="results", bufs=8))
+        psum = ctx.enter_context(tc.psum_pool(name="psum", bufs=4))
         ctx.enter_context(tc.manual_schedule())
 
         identity = resident.tile([P, P], F32)
         make_identity(nc, identity[:])
 
-        inputs = {"phi": (x_2, phi_w, phi_b), "theta": (x, theta_w, theta_b)}
-        pieces = CONFIG["pieces"]
-        raw = {}
-        for i, (b, side, first, width) in enumerate(pieces):
-            tile = resident.tile([P, PASSES, PACK, width], BF16, name="raw_%d" % i)
-            raw[i] = tile
         w_raw, bias, w_grouped, weight = {}, {}, {}, {}
         for side in ("phi", "theta"):
-            w_raw_tile = resident.tile([P, PACK, CHANNELS], BF16, name="%s_w_raw" % side)
-            bias_tile = resident.tile([P, PACK], BF16, name="%s_bias" % side)
-            grouped_tile = resident.tile([P, PASSES, PACK, P, PACK], BF16, name="%s_w_grouped" % side, align_bytes=64)
-            codes = resident.tile([P, PASSES, INNER], U32, name="%s_w_codes" % side, align_bytes=64)
-            scales = resident.tile([P, PASSES, INNER], U8, name="%s_w_scales" % side, align_bytes=64)
-            w_raw[side], bias[side], w_grouped[side], weight[side] = w_raw_tile, bias_tile, grouped_tile, (codes, scales)
-            nc.scalar.dma_start(out=bias_tile[:], in_=inputs[side][2].rearrange("(m t) -> m t", t=PACK))
+            w_raw[side] = resident.tile([P, PACK, CHANNELS], BF16, name="%s_w_raw" % side)
+            bias[side] = resident.tile([P, PACK], BF16, name="%s_bias" % side)
+            w_grouped[side] = resident.tile(
+                [P, PASSES, PACK, P, PACK], BF16, name="%s_w_grouped" % side, align_bytes=64
+            )
+            weight[side] = (
+                resident.tile([P, PASSES, INNER], U32, name="%s_w_codes" % side, align_bytes=64),
+                resident.tile([P, PASSES, INNER], U8, name="%s_w_scales" % side, align_bytes=64),
+            )
+            nc.scalar.dma_start(out=bias[side][:], in_=inputs[side][2].rearrange("(m t) -> m t", t=PACK))
+        raw = {}
 
-        for step in CONFIG["loads"]:
-            if step[0] == "w":
-                side, half = step[1], step[2]
-                ks = slice(half * K_PASS, (half + 1) * K_PASS)
-                nc.sync.dma_start(
-                    out=w_raw[side][:, :, ks],
-                    in_=inputs[side][1].rearrange("(m t) k -> m t k", t=PACK)[:, :, ks],
-                )
-            elif step[0] == "W":
-                side = step[1]
-                nc.sync.dma_start(out=w_raw[side][:], in_=inputs[side][1].rearrange("(m t) k -> m t k", t=PACK))
-            else:
-                i, c = step[1], step[2]
-                b, side, first, width = pieces[i]
-                load_points(nc, raw[i], inputs[side][0][b], c, first, width)
+        def load_points(b, side, first, width):
+            tile = resident.tile([P, PASSES, PACK, width], BF16, name="raw_%s_%d_%d" % (side, b, first))
+            for c in range(PASSES):
+                rows = inputs[side][0][b, c * K_PASS : (c + 1) * K_PASS, first : first + width]
+                nc.sync.dma_start(out=tile[:, c], in_=rows.rearrange("(p j) n -> p j n", j=PACK))
+            for i, piece in enumerate(PIECES):
+                if piece[:2] == (b, side) and first <= piece[2] < first + width:
+                    raw[i] = tile[:, :, :, piece[2] - first : piece[2] - first + piece[3]]
 
-        quantised, projected, grouped, points = {}, {}, {}, {}
-        jobs = []
+        def load_weights(side):
+            nc.sync.dma_start(out=w_raw[side][:], in_=inputs[side][1].rearrange("(m t) k -> m t k", t=PACK))
 
-        def get_grouped(i):
+        load_points(0, "phi", 0, 512)
+        load_weights("phi")
+        load_points(0, "theta", 0, 512)
+        load_weights("theta")
+        load_points(0, "phi", 512, 512)
+        load_points(0, "theta", 512, 512)
+        load_points(1, "phi", 0, POINTS)
+        load_points(1, "theta", 0, POINTS)
+
+        grouped = {}
+
+        def regroup(engine, i, c, lo, hi):
+            if lo == hi:
+                return
             if i not in grouped:
-                width = pieces[i][3]
-                tile = stage.tile([P, PASSES, width, PACK], BF16, name="points_grouped_%d" % width, align_bytes=64)
-                grouped[i] = tile
-            return grouped[i]
+                grouped[i] = stage.tile(
+                    [P, PASSES, PIECES[i][3], PACK],
+                    BF16,
+                    name="points_grouped_%d" % i,
+                    tag="points_grouped",
+                    bufs=2,
+                    align_bytes=64,
+                )
+            views = side_by_side(raw[i][:, c, :, lo:hi], grouped[i][:, c, lo:hi])
+            if engine == "vector":
+                nc.vector.tensor_copy(**views)
+            elif engine == "scalar":
+                nc.scalar.copy(**views)
+            else:
+                nc.gpsimd.tensor_scalar(
+                    out=views["out"], in0=views["in_"], scalar1=1.0, scalar2=0.0, op0=MULT, op1=ADD
+                )
 
-        def x1(i, c, engine, lo=0, hi=None):
-            hi = pieces[i][3] if hi is None else hi
-            if hi > lo:
-                regroup(nc, engine, raw[i][:, c, :, lo:hi], get_grouped(i)[:, c, lo:hi])
+        points = {}
 
-        def q(i):
-            width = pieces[i][3]
+        def quantise_points(i):
+            width = PIECES[i][3]
             codes = stage.tile([P, PASSES, width], U32, name="points_codes_%d" % width, align_bytes=64)
             scales = stage.tile([P, PASSES, width], U8, name="points_scales_%d" % width, align_bytes=64)
             points[i] = (codes, scales)
-            nc.vector.quantize_mx(
-                out=codes[:].rearrange("p c n -> p (c n)").bitcast(FP8X4),
-                scales=scales[:].rearrange("p c n -> p (c n)"),
-                in_=grouped[i][:].rearrange("p c n j -> p (c n j)"),
+            quantise(
+                nc,
+                codes[:].rearrange("p c n -> p (c n)"),
+                scales[:].rearrange("p c n -> p (c n)"),
+                grouped[i][:].rearrange("p c n j -> p (c n) j"),
             )
 
-        pg = {}
+        def quantise_weights(side):
+            codes, scales = weight[side]
+            quantise(
+                nc,
+                codes[:].rearrange("p c n -> p (c n)"),
+                scales[:].rearrange("p c n -> p (c n)"),
+                w_grouped[side][:].rearrange("p c t m j -> p (c t m) j"),
+            )
 
-        def banks(i):
-            return pieces[i][3] // P
+        projection = {}
 
-        def pj(i, k):
-            b, side, first, width = pieces[i]
+        def project(i, k):
+            side = PIECES[i][1]
             w_codes, w_scales = weight[side]
             codes, scales = points[i]
-            acc = psum.tile([P, PACK, P], F32, tag="projection", bufs=4, name="acc_projection")
-            projected[i, k] = acc
-            cols = slice(k * P, (k + 1) * P)
+            acc = psum.tile([P, PACK, P], F32, tag="projection", name="projection")
+            projection[i, k] = acc
+            columns = slice(k * P, (k + 1) * P)
             for t in range(PACK):
+                rows = slice(t * P, (t + 1) * P)
                 for c in range(PASSES):
                     nc.tensor.matmul_mx(
                         out=acc[:, t, :],
-                        lhsT=w_codes[:, c, t * P : (t + 1) * P].bitcast(FP8X4),
-                        lhsT_scale=w_scales[:, c, t * P : (t + 1) * P],
-                        rhs=codes[:, c, cols].bitcast(FP8X4),
-                        rhs_scale=scales[:, c, cols],
+                        lhsT=w_codes[:, c, rows].bitcast(FP8X4),
+                        lhsT_scale=w_scales[:, c, rows],
+                        rhs=codes[:, c, columns].bitcast(FP8X4),
+                        rhs_scale=scales[:, c, columns],
                         start=(c == 0),
                         stop=(c == PASSES - 1),
                     )
 
-        def pjd(i, k):
-            b, side, first, width = pieces[i]
+        projected = {}
+
+        def add_bias(i, k):
+            side, width = PIECES[i][1], PIECES[i][3]
             if k == 0:
-                tile = stage.tile([P, width, PACK], BF16, name="projected_grouped_%d" % width, align_bytes=64)
-                pg[i] = tile
+                projected[i] = stage.tile([P, width, PACK], BF16, name="projected_%d" % width, align_bytes=64)
             nc.vector.tensor_tensor(
-                out=pg[i][:, k * P : (k + 1) * P, :],
-                in0=projected[i, k][:].rearrange("p t n -> p n t"),
+                out=projected[i][:, k * P : (k + 1) * P, :],
+                in0=projection[i, k][:].rearrange("p t n -> p n t"),
                 in1=bias[side][:].unsqueeze(1).to_broadcast([P, P, PACK]),
-                op=mybir.AluOpType.add,
+                op=ADD,
             )
 
-        done = {}
+        quantised, done, blocks = {}, {}, []
 
-        def qp(i):
-            b, side, first, width = pieces[i]
+        def quantise_projection(i):
+            b, side, first, width = PIECES[i]
             if (side, b) not in quantised:
-                codes = keep.tile([P, POINTS], U32, name="%s_codes" % side, align_bytes=64)
-                scales = keep.tile([P, POINTS], U8, name="%s_scales" % side, align_bytes=64)
-                quantised[side, b] = (codes, scales)
-                done[side, b] = []
-            quantise_projection(nc, pg[i], quantised[side, b], slice(first, first + width))
-            done[side, b].append((first, width))
-            other = "theta" if side == "phi" else "phi"
-            ranges = sorted(done.get((other, b), []))
-            merged = []
-            for f, w in ranges:
-                if merged and merged[-1][1] == f and f % BANK:
-                    merged[-1] = (merged[-1][0], f + w)
-                else:
-                    merged.append((f, f + w))
-            if side == "phi":
-                for f, e in merged:
-                    for row in range(f, e, P):
-                        jobs.append((b, row, first, width))
+                quantised[side, b] = (
+                    stage.tile([P, POINTS], U32, name="%s_codes" % side, align_bytes=64),
+                    stage.tile([P, POINTS], U8, name="%s_scales" % side, align_bytes=64),
+                )
+                done[side, b] = 0
+            codes, scales = quantised[side, b]
+            columns = slice(first, first + width)
+            quantise(nc, codes[:, columns], scales[:, columns], projected[i][:])
+            done[side, b] = first + width
+            rows, cols = range(done.get(("theta", b), 0)), range(done.get(("phi", b), 0))
+            if side == "theta":
+                rows = range(first, first + width)
             else:
-                for row in range(first, first + width, P):
-                    for f, e in merged:
-                        jobs.append((b, row, f, e - f))
+                cols = range(first, first + width)
+            for row in rows[::P]:
+                for column in cols[::BANK]:
+                    blocks.append((b, row, column, min(BANK, cols.stop - column)))
 
-        def jobs_run(n, engines):
-            for k in range(min(n, len(jobs))):
-                b, row, column, width = jobs[0]
-                jobs.remove(jobs[0])
-                affinity(nc, results, psum, quantised["theta", b], quantised["phi", b], row, column, width, out[b], engines[k % len(engines)])
+        def affinity(count, engines):
+            for k in range(min(count, len(blocks))):
+                b, row, column, width = blocks[0]
+                blocks.remove(blocks[0])
+                theta_codes, theta_scales = quantised["theta", b]
+                phi_codes, phi_scales = quantised["phi", b]
+                rows, columns = slice(row, row + P), slice(column, column + width)
+                acc = psum.tile([P, width], F32, tag="product", name="product")
+                nc.tensor.matmul_mx(
+                    out=acc[:],
+                    lhsT=theta_codes[:, rows].bitcast(FP8X4),
+                    lhsT_scale=theta_scales[:, rows],
+                    rhs=phi_codes[:, columns].bitcast(FP8X4),
+                    rhs_scale=phi_scales[:, columns],
+                    start=True,
+                    stop=True,
+                )
+                result = results.tile([P, width], F32, name="result_%d" % width)
+                if engines[k % len(engines)] == "vector":
+                    nc.vector.tensor_scalar_mul(out=result[:], in0=acc[:], scalar1=1.0 / POINTS)
+                else:
+                    nc.scalar.mul(out=result[:], in_=acc[:], mul=1.0 / POINTS)
+                nc.sync.dma_start(out=out[b, rows, columns], in_=result[:])
 
-        def wt(side, c, eng="SS"):
-            transpose_weights(nc, psum, identity, w_raw[side], w_grouped[side], c, eng)
+        by_gpsimd = [0, 0, 512, 192, 448, 448, 448, 256, 256]
 
-        def wq(side):
-            codes, scales = weight[side]
-            nc.vector.quantize_mx(
-                out=codes[:].rearrange("p c n -> p (c n)").bitcast(FP8X4),
-                scales=scales[:].rearrange("p c n -> p (c n)"),
-                in_=w_grouped[side][:].rearrange("p c t m j -> p (c t m j)"),
-            )
+        def regroup_later(i):
+            width = PIECES[i][3]
+            regroup("gpsimd", i, 0, 0, by_gpsimd[i])
+            regroup("scalar", i, 1, 0, width)
+            regroup("scalar", i, 0, by_gpsimd[i], width)
 
-
-        CFG = CONFIG
-        gs, ss, qa, qk, qb, ea, ek, eb = [CFG[k] for k in ("g", "s", "qa", "qk", "qb", "ea", "ek", "eb")]
-        n = len(pieces)
-
-        def xg(i):
-            x1(i, 0, "G", 0, gs[i])
-
-        def xs(i):
-            w = pieces[i][3]
-            x1(i, 1, "S", w - ss[i], w)
-
-        def xv(i):
-            w = pieces[i][3]
-            x1(i, 0, "V", gs[i], w)
-            x1(i, 1, "V", 0, w - ss[i])
-
-        xg(0)
-        xs(0)
-        xv(0)
-        wt("phi", 0, CFG["we"][0])
-        wt("phi", 1, CFG["we"][1])
-        xg(1)
-        xs(1)
-        q(0)
-        xv(1)
-        wq("phi")
-        wt("theta", 0, CFG["we"][2])
-        wt("theta", 1, CFG["we"][3])
+        regroup("vector", 0, 0, 0, 512)
+        regroup("vector", 0, 1, 0, 512)
+        quantise_points(0)
+        transpose_weights(nc, psum, identity, w_raw["phi"], w_grouped["phi"], ("vector", "scalar"))
+        quantise_weights("phi")
         for k in range(banks(0)):
-            pj(0, k)
-        xg(2)
-        xs(2)
-        for i in range(1, n + 2):
-            if i < n:
-                q(i)
-            if i == 1:
-                wq("theta")
-            jobs_run(qa[i], ea[i])
-            if i + 2 < n and i > 0:
-                xg(i + 2)
-            for k in range(4):
-                if i - 1 < n and k < banks(i - 1):
-                    pjd(i - 1, k)
-                if i < n and k < banks(i):
-                    pj(i, k)
-                jobs_run(qk[i], ek[i])
-            if i + 2 < n and i > 0:
-                xs(i + 2)
-            if i + 1 < n:
-                xv(i + 1)
-            if i - 1 < n:
-                qp(i - 1)
-            jobs_run(qb[i], eb[i])
+            project(0, k)
+        regroup("scalar", 1, 1, 0, 512)
+        regroup("vector", 1, 0, 0, 512)
+        quantise_points(1)
+        for k in range(banks(0)):
+            add_bias(0, k)
+        transpose_weights(nc, psum, identity, w_raw["theta"], w_grouped["theta"], ("scalar", "vector"))
+        regroup_later(2)
+        quantise_weights("theta")
+        for k in range(banks(1)):
+            project(1, k)
+        regroup_later(3)
+        quantise_projection(0)
+        for i in range(HEAD, LAST + 1):
+            if i < LAST:
+                quantise_points(i)
+            if HEAD < i <= LAG_UNTIL:
+                quantise_projection(i - 2)
+                affinity(3, ("scalar",))
+            if i + 2 < LAST:
+                regroup_later(i + 2)
+            for k in range(BANK // P):
+                if k < banks(i - 1):
+                    add_bias(i - 1, k)
+                if i < LAST and k < banks(i):
+                    project(i, k)
+                if k < 3:
+                    affinity(1, ("scalar",))
+            if i >= LAG_UNTIL:
+                quantise_projection(i - 1)
+                affinity(12, ("scalar",) if i < LAST else ("scalar", "vector"))

@@ -84,6 +84,14 @@ def tile_sgcam_pa_kernel(tc, x, x_2, theta_w, theta_b, phi_w, phi_b, out):
 
         identity = resident.tile([P, P], F32)
         make_identity(nc, identity[:])
+        zeros = resident.tile([P, BANK], BF16)
+        nc.gpsimd.memset(zeros[:], 0.0)
+
+        def keep_busy(count):
+            for k in range(count):
+                unread = psum.tile([P, BANK], F32, tag="product", name="unread")
+                nc.tensor.matmul(unread[:], zeros[:, :P], zeros[:], start=True, stop=True)
+
 
         w_raw, bias, w_grouped, weight = {}, {}, {}, {}
         for side in ("phi", "theta"):
@@ -261,6 +269,7 @@ def tile_sgcam_pa_kernel(tc, x, x_2, theta_w, theta_b, phi_w, phi_b, out):
         regroup("vector", 0, 1, 0, 512)
         quantise_points(0)
         transpose_weights(nc, psum, identity, w_raw["phi"], w_grouped["phi"], ("vector", "scalar"))
+        keep_busy(4)
         quantise_weights("phi")
         for k in range(banks(0)):
             project(0, k)

@@ -280,6 +280,7 @@ def tile_sgcam_pa_kernel(tc, x, x_2, theta_w, theta_b, phi_w, phi_b, out):
             add_bias(0, k)
         transpose_weights(nc, psum, identity, w_raw["theta"], w_grouped["theta"], ("scalar", "vector"))
         regroup_later(2)
+        keep_busy(4)
         quantise_weights("theta")
         for k in range(banks(1)):
             project(1, k)

@@ -50,7 +50,7 @@ def side_by_side(rows_apart, together):
 
 
 def transpose_weights(nc, psum, identity, w_raw, grouped, engines):
-    words = w_raw[:].bitcast(F32).rearrange("m t (c p u) -> m t c u p", c=PASSES, u=PACK // WORD)
+    words = w_raw[:].bitcast(F32).rearrange("m t (c u p) -> m t c u p", c=PASSES, u=PACK // WORD)
     grouped_words = grouped[:].bitcast(F32)
     for c in range(PASSES):
         for first in range(0, PACK, 2):
@@ -110,8 +110,12 @@ def tile_sgcam_pa_kernel(tc, x, x_2, theta_w, theta_b, phi_w, phi_b, out):
         def load_points(b, side, first, width):
             tile = resident.tile([P, PASSES, PACK, width], BF16, name="raw_%s_%d_%d" % (side, b, first))
             for c in range(PASSES):
-                rows = inputs[side][0][b, c * K_PASS : (c + 1) * K_PASS, first : first + width]
-                nc.sync.dma_start(out=tile[:, c], in_=rows.rearrange("(p j) n -> p j n", j=PACK))
+                for u in range(PACK // WORD):
+                    top = c * K_PASS + u * WORD * P
+                    rows = inputs[side][0][b, top : top + WORD * P, first : first + width]
+                    nc.sync.dma_start(
+                        out=tile[:, c, u * WORD : (u + 1) * WORD], in_=rows.rearrange("(p e) n -> p e n", e=WORD)
+                    )
             for i, piece in enumerate(PIECES):
                 if piece[:2] == (b, side) and first <= piece[2] < first + width:
                     raw[i] = tile[:, :, :, piece[2] - first : piece[2] - first + piece[3]]

@@ -129,8 +129,10 @@ def tile_sgcam_pa_kernel(tc, x, x_2, theta_w, theta_b, phi_w, phi_b, out):
         load_weights("theta")
         load_points(0, "phi", 512, 512)
         load_points(0, "theta", 512, 512)
-        load_points(1, "phi", 0, POINTS)
-        load_points(1, "theta", 0, POINTS)
+        load_points(1, "phi", 0, 512)
+        load_points(1, "theta", 0, 512)
+        load_points(1, "phi", 512, 512)
+        load_points(1, "theta", 512, 512)
 
         grouped = {}
 
@@ -261,12 +263,14 @@ def tile_sgcam_pa_kernel(tc, x, x_2, theta_w, theta_b, phi_w, phi_b, out):
                     nc.scalar.mul(out=result[:], in_=acc[:], mul=1.0 / POINTS)
                 nc.sync.dma_start(out=out[b, rows, columns], in_=result[:])
 
-        by_gpsimd = [0, 0, 512, 192, 448, 448, 448, 256, 256]
+        by_gpsimd = [0, 0, 448, 0, 448, 448, 448, 256, 256]
 
         def regroup_later(i):
             width = PIECES[i][3]
             regroup("gpsimd", i, 0, 0, by_gpsimd[i])
-            regroup("scalar", i, 1, 0, width)
+            more = {7: 128, 8: 128}.get(i, 0)
+            regroup("gpsimd", i, 1, 0, more)
+            regroup("scalar", i, 1, more, width)
             regroup("scalar", i, 0, by_gpsimd[i], width)
 
         regroup("vector", 0, 0, 0, 512)
@@ -275,21 +279,26 @@ def tile_sgcam_pa_kernel(tc, x, x_2, theta_w, theta_b, phi_w, phi_b, out):
         transpose_weights(nc, psum, identity, w_raw["phi"], w_grouped["phi"], ("vector", "scalar"))
         keep_busy(4)
         quantise_weights("phi")
-        for k in range(banks(0)):
+        for k in range(2):
             project(0, k)
-        regroup("scalar", 1, 1, 0, 512)
+        regroup("scalar", 1, 1, 128, 512)
         regroup("vector", 1, 0, 0, 512)
+        regroup("vector", 1, 1, 0, 128)
         quantise_points(1)
+        transpose_weights(nc, psum, identity, w_raw["theta"], w_grouped["theta"], ("scalar", "scalar"))
+        for k in range(2, banks(0)):
+            project(0, k)
         for k in range(banks(0)):
             add_bias(0, k)
-        transpose_weights(nc, psum, identity, w_raw["theta"], w_grouped["theta"], ("scalar", "vector"))
         regroup_later(2)
         keep_busy(4)
         quantise_weights("theta")
         for k in range(banks(1)):
             project(1, k)
-        regroup_later(3)
+        regroup("scalar", 3, 1, 0, 512)
+        regroup("scalar", 3, 0, 192, 512)
         quantise_projection(0)
+        regroup("vector", 3, 0, 0, 192)
         for i in range(HEAD, LAST + 1):
             if i < LAST:
                 quantise_points(i)

@@ -104,7 +104,6 @@ def tile_sgcam_pa_kernel(tc, x, x_2, theta_w, theta_b, phi_w, phi_b, out):
                 resident.tile([P, PASSES, INNER], U32, name="%s_w_codes" % side, align_bytes=64),
                 resident.tile([P, PASSES, INNER], U8, name="%s_w_scales" % side, align_bytes=64),
             )
-            nc.scalar.dma_start(out=bias[side][:], in_=inputs[side][2].rearrange("(m t) -> m t", t=PACK))
         raw = {}
 
         def load_points(b, side, first, width):
@@ -127,6 +126,8 @@ def tile_sgcam_pa_kernel(tc, x, x_2, theta_w, theta_b, phi_w, phi_b, out):
         load_weights("phi")
         load_points(0, "theta", 0, 512)
         load_weights("theta")
+        for side in ("phi", "theta"):
+            nc.sync.dma_start(out=bias[side][:], in_=inputs[side][2].rearrange("(m t) -> m t", t=PACK))
         load_points(0, "phi", 512, 512)
         load_points(0, "theta", 512, 512)
         load_points(1, "phi", 0, 512)

from contextlib import ExitStack

import concourse.mybir as mybir
from concourse.masks import make_identity

FP8X4 = mybir.dt.float8_e4m3fn_x4
BF16 = mybir.dt.bfloat16
F32 = mybir.dt.float32
U32 = mybir.dt.uint32
U8 = mybir.dt.uint8
ADD = mybir.AluOpType.add
MULT = mybir.AluOpType.mult

BATCH, CHANNELS, INNER, POINTS = 2, 1024, 512, 1024

P = 128
PACK = 4
K_PASS = P * PACK
PASSES = CHANNELS // K_PASS
WORD = 2
BANK = 512

FLOPS = 2 * BATCH * (2 * INNER * CHANNELS * POINTS + POINTS * POINTS * INNER)

PIECES = [
    (0, "phi", 0, 512),
    (0, "theta", 0, 512),
    (0, "phi", 512, 512),
    (0, "theta", 512, 512),
    (1, "phi", 0, 512),
    (1, "theta", 0, 512),
    (1, "phi", 512, 512),
    (1, "theta", 512, 256),
    (1, "theta", 768, 256),
]
LAST = len(PIECES)
HEAD = 2
LAG_UNTIL = 7


def banks(i):
    return PIECES[i][3] // P


def side_by_side(rows_apart, together):
    return {
        "out": together.rearrange("p (g i) j -> p g j i", i=4),
        "in_": rows_apart.rearrange("p j (g i) -> p g j i", i=4),
    }


def transpose_weights(nc, psum, identity, w_raw, grouped, engines):
    words = w_raw[:].bitcast(F32).rearrange("m t (c u p) -> m t c u p", c=PASSES, u=PACK // WORD)
    grouped_words = grouped[:].bitcast(F32)
    for c in range(PASSES):
        for first in range(0, PACK, 2):
            flipped = psum.tile([P, 2, PACK // WORD, P], F32, tag="product", name="flipped")
            for t in range(2):
                for u in range(PACK // WORD):
                    nc.tensor.transpose(flipped[:, t, u, :], words[:, first + t, c, u, :], identity[:])
            out = grouped_words[:, c, first : first + 2]
            in_ = flipped[:].rearrange("p t u m -> p t m u")
            if engines[first // 2] == "vector":
                nc.vector.tensor_copy(out=out, in_=in_)
            else:
                nc.scalar.copy(out=out, in_=in_)


def quantise(nc, codes, scales, values):
    nc.vector.quantize_mx(
        out=codes.bitcast(FP8X4), scales=scales, in_=values.rearrange("p n j -> p (n j)")
    )


def tile_sgcam_pa_kernel(tc, x, x_2, theta_w, theta_b, phi_w, phi_b, out):
    nc = tc.nc
    inputs = {"phi": (x_2, phi_w, phi_b), "theta": (x, theta_w, theta_b)}
    with ExitStack() as ctx:
        resident = ctx.enter_context(tc.tile_pool(name="resident", bufs=1))
        stage = ctx.enter_context(tc.tile_pool(name="stage", bufs=2))
        results = ctx.enter_context(tc.tile_pool(name="results", bufs=8))
        psum = ctx.enter_context(tc.psum_pool(name="psum", bufs=4))
        ctx.enter_context(tc.manual_schedule())

        identity = resident.tile([P, P], F32)
        make_identity(nc, identity[:])
        zeros = resident.tile([P, BANK], BF16)
        nc.gpsimd.memset(zeros[:], 0.0)

        def keep_busy(count):
            for k in range(count):
                unread = psum.tile([P, BANK], F32, tag="product", name="unread")
                nc.tensor.matmul(unread[:], zeros[:, :P], zeros[:], start=True, stop=True)


        w_raw, bias, w_grouped, weight = {}, {}, {}, {}
        for side in ("phi", "theta"):
            w_raw[side] = resident.tile([P, PACK, CHANNELS], BF16, name="%s_w_raw" % side)
            bias[side] = resident.tile([P, PACK], BF16, name="%s_bias" % side)
            w_grouped[side] = resident.tile(
                [P, PASSES, PACK, P, PACK], BF16, name="%s_w_grouped" % side, align_bytes=64
            )
            weight[side] = (
                resident.tile([P, PASSES, INNER], U32, name="%s_w_codes" % side, align_bytes=64),
                resident.tile([P, PASSES, INNER], U8, name="%s_w_scales" % side, align_bytes=64),
            )
        raw = {}

        def load_points(b, side, first, width):
            tile = resident.tile([P, PASSES, PACK, width], BF16, name="raw_%s_%d_%d" % (side, b, first))
            for c in range(PASSES):
                for u in range(PACK // WORD):
                    top = c * K_PASS + u * WORD * P
                    rows = inputs[side][0][b, top : top + WORD * P, first : first + width]
                    nc.sync.dma_start(
                        out=tile[:, c, u * WORD : (u + 1) * WORD], in_=rows.rearrange("(p e) n -> p e n", e=WORD)
                    )
            for i, piece in enumerate(PIECES):
                if piece[:2] == (b, side) and first <= piece[2] < first + width:
                    raw[i] = tile[:, :, :, piece[2] - first : piece[2] - first + piece[3]]

        def load_weights(side):
            nc.sync.dma_start(out=w_raw[side][:], in_=inputs[side][1].rearrange("(m t) k -> m t k", t=PACK))

        load_points(0, "phi", 0, 512)
        load_weights("phi")
        load_points(0, "theta", 0, 512)
        load_weights("theta")
        for side in ("phi", "theta"):
            nc.sync.dma_start(out=bias[side][:], in_=inputs[side][2].rearrange("(m t) -> m t", t=PACK))
        load_points(0, "phi", 512, 512)
        load_points(0, "theta", 512, 512)
        load_points(1, "phi", 0, 512)
        load_points(1, "theta", 0, 512)
        load_points(1, "phi", 512, 512)
        load_points(1, "theta", 512, 512)

        grouped = {}

        def regroup(engine, i, c, lo, hi):
            if lo == hi:
                return
            if i not in grouped:
                grouped[i] = stage.tile(
                    [P, PASSES, PIECES[i][3], PACK],
                    BF16,
                    name="points_grouped_%d" % i,
                    tag="points_grouped",
                    bufs=2,
                    align_bytes=64,
                )
            views = side_by_side(raw[i][:, c, :, lo:hi], grouped[i][:, c, lo:hi])
            if engine == "vector":
                nc.vector.tensor_copy(**views)
            elif engine == "scalar":
                nc.scalar.copy(**views)
            else:
                nc.gpsimd.tensor_scalar(
                    out=views["out"], in0=views["in_"], scalar1=1.0, scalar2=0.0, op0=MULT, op1=ADD
                )

        points = {}

        def quantise_points(i):
            width = PIECES[i][3]
            codes = stage.tile([P, PASSES, width], U32, name="points_codes_%d" % width, align_bytes=64)
            scales = stage.tile([P, PASSES, width], U8, name="points_scales_%d" % width, align_bytes=64)
            points[i] = (codes, scales)
            quantise(
                nc,
                codes[:].rearrange("p c n -> p (c n)"),
                scales[:].rearrange("p c n -> p (c n)"),
                grouped[i][:].rearrange("p c n j -> p (c n) j"),
            )

        def quantise_weights(side):
            codes, scales = weight[side]
            quantise(
                nc,
                codes[:].rearrange("p c n -> p (c n)"),
                scales[:].rearrange("p c n -> p (c n)"),
                w_grouped[side][:].rearrange("p c t m j -> p (c t m) j"),
            )

        projection = {}

        def project(i, k):
            side = PIECES[i][1]
            w_codes, w_scales = weight[side]
            codes, scales = points[i]
            acc = psum.tile([P, PACK, P], F32, tag="projection", name="projection")
            projection[i, k] = acc
            columns = slice(k * P, (k + 1) * P)
            for t in range(PACK):
                rows = slice(t * P, (t + 1) * P)
                for c in range(PASSES):
                    nc.tensor.matmul_mx(
                        out=acc[:, t, :],
                        lhsT=w_codes[:, c, rows].bitcast(FP8X4),
                        lhsT_scale=w_scales[:, c, rows],
                        rhs=codes[:, c, columns].bitcast(FP8X4),
                        rhs_scale=scales[:, c, columns],
                        start=(c == 0),
                        stop=(c == PASSES - 1),
                    )

        projected = {}

        def add_bias(i, k):
            side, width = PIECES[i][1], PIECES[i][3]
            if k == 0:
                projected[i] = stage.tile([P, width, PACK], BF16, name="projected_%d" % width, align_bytes=64)
            nc.vector.tensor_tensor(
                out=projected[i][:, k * P : (k + 1) * P, :],
                in0=projection[i, k][:].rearrange("p t n -> p n t"),
                in1=bias[side][:].unsqueeze(1).to_broadcast([P, P, PACK]),
                op=ADD,
            )

        quantised, done, blocks = {}, {}, []

        def quantise_projection(i):
            b, side, first, width = PIECES[i]
            if (side, b) not in quantised:
                quantised[side, b] = (
                    stage.tile([P, POINTS], U32, name="%s_codes" % side, align_bytes=64),
                    stage.tile([P, POINTS], U8, name="%s_scales" % side, align_bytes=64),
                )
                done[side, b] = 0
            codes, scales = quantised[side, b]
            columns = slice(first, first + width)
            quantise(nc, codes[:, columns], scales[:, columns], projected[i][:])
            done[side, b] = first + width
            rows, cols = range(done.get(("theta", b), 0)), range(done.get(("phi", b), 0))
            if side == "theta":
                rows = range(first, first + width)
            else:
                cols = range(first, first + width)
            for row in rows[::P]:
                for column in cols[::BANK]:
                    blocks.append((b, row, column, min(BANK, cols.stop - column)))

        def affinity(count, engines):
            for k in range(min(count, len(blocks))):
                b, row, column, width = blocks[0]
                blocks.remove(blocks[0])
                theta_codes, theta_scales = quantised["theta", b]
                phi_codes, phi_scales = quantised["phi", b]
                rows, columns = slice(row, row + P), slice(column, column + width)
                acc = psum.tile([P, width], F32, tag="product", name="product")
                nc.tensor.matmul_mx(
                    out=acc[:],
                    lhsT=theta_codes[:, rows].bitcast(FP8X4),
                    lhsT_scale=theta_scales[:, rows],
                    rhs=phi_codes[:, columns].bitcast(FP8X4),
                    rhs_scale=phi_scales[:, columns],
                    start=True,
                    stop=True,
                )
                result = results.tile([P, width], F32, name="result_%d" % width)
                if engines[k % len(engines)] == "vector":
                    nc.vector.tensor_scalar_mul(out=result[:], in0=acc[:], scalar1=1.0 / POINTS)
                else:
                    nc.scalar.mul(out=result[:], in_=acc[:], mul=1.0 / POINTS)
                nc.sync.dma_start(out=out[b, rows, columns], in_=result[:])

        by_gpsimd = [0, 0, 448, 0, 448, 448, 448, 256, 256]

        def regroup_later(i):
            width = PIECES[i][3]
            regroup("gpsimd", i, 0, 0, by_gpsimd[i])
            more = {7: 128, 8: 128}.get(i, 0)
            regroup("gpsimd", i, 1, 0, more)
            regroup("scalar", i, 1, more, width)
            regroup("scalar", i, 0, by_gpsimd[i], width)

        regroup("vector", 0, 0, 0, 512)
        regroup("vector", 0, 1, 0, 512)
        quantise_points(0)
        transpose_weights(nc, psum, identity, w_raw["phi"], w_grouped["phi"], ("vector", "scalar"))
        keep_busy(4)
        quantise_weights("phi")
        for k in range(2):
            project(0, k)
        regroup("scalar", 1, 1, 128, 512)
        regroup("vector", 1, 0, 0, 512)
        regroup("vector", 1, 1, 0, 128)
        quantise_points(1)
        transpose_weights(nc, psum, identity, w_raw["theta"], w_grouped["theta"], ("scalar", "scalar"))
        for k in range(2, banks(0)):
            project(0, k)
        for k in range(banks(0)):
            add_bias(0, k)
        regroup_later(2)
        keep_busy(4)
        quantise_weights("theta")
        for k in range(banks(1)):
            project(1, k)
        regroup("scalar", 3, 1, 0, 512)
        regroup("scalar", 3, 0, 192, 512)
        quantise_projection(0)
        regroup("vector", 3, 0, 0, 192)
        for i in range(HEAD, LAST + 1):
            if i < LAST:
                quantise_points(i)
            if HEAD < i <= LAG_UNTIL:
                quantise_projection(i - 2)
                affinity(3, ("scalar",))
            if i + 2 < LAST:
                regroup_later(i + 2)
            for k in range(BANK // P):
                if k < banks(i - 1):
                    add_bias(i - 1, k)
                if i < LAST and k < banks(i):
                    project(i, k)
                if k < 3:
                    affinity(1, ("scalar",))
            if i >= LAG_UNTIL:
                quantise_projection(i - 1)
                affinity(12, ("scalar",) if i < LAST else ("scalar", "vector"))
